import numpy as np
import ml_dtypes


def mxq(x, axis, fmt="e4m3"):
    dtype, down = {"e4m3": (ml_dtypes.float8_e4m3fn, 7), "e5m2": (ml_dtypes.float8_e5m2, 14)}[fmt]
    v = np.moveaxis(np.asarray(x, np.float32).astype(ml_dtypes.bfloat16).astype(np.float64), axis, -1)
    blocks = v.reshape(v.shape[:-1] + (-1, 32))
    amax = np.abs(blocks).max(-1, keepdims=True)
    byte = np.maximum(np.where(amax > 0, np.frexp(amax)[1] - 1 + 127, 0) - down, 1)
    scale = np.exp2(byte - 127.0)
    codes = (blocks / scale).astype(np.float32).astype(dtype).astype(np.float64)
    return np.moveaxis((codes * scale).reshape(v.shape), -1, axis)


WIDE = False


def mx_kscale(k):
    if not WIDE:
        return np.ones(k)
    levels = np.array([20, -20, 10, -10, 0])
    a = np.random.permutation(np.resize(levels, k // 512 * 4)).reshape(k // 512, 4)
    idx = np.arange(k)
    return np.exp2(a[idx // 512, idx % 128 // 32])


BF16 = ml_dtypes.bfloat16


def bf(x):
    return np.asarray(x, np.float32).astype(BF16)


def f64(x):
    return np.asarray(x).astype(np.float64)


B, D, U = 2048, 512, 512
GATES = ["i", "f", "c", "o"]


def sigmoid(v):
    return 1.0 / (1.0 + np.exp(-v))


def setup_inputs():
    u = mx_kscale(U)
    inp = {"inputs": bf(np.random.standard_normal((B, D))),
           "h": bf(np.random.standard_normal((B, U))),
           "c": bf(np.random.standard_normal((B, U)))}
    for g in GATES:
        inp["w_" + g] = bf(np.random.standard_normal((D, U)) * 1.1 / np.sqrt(D))
        inp["u_" + g] = bf(np.random.standard_normal((U, U)) * 1.1 / np.sqrt(U))
        inp["b_" + g] = bf(np.random.standard_normal(U) * 0.2)
    go = bf(np.random.standard_normal((B, U)) * np.exp2(np.random.randint(-12, 1, (B, 1))) * 32.0 * u)
    z = np.concatenate([f64(inp["inputs"]) @ f64(inp["w_" + g]) + f64(inp["h"]) @ f64(inp["u_" + g]) + f64(inp["b_" + g])
                        for g in GATES], axis=1)
    for g in GATES:
        inp["w_" + g] = bf(f64(inp["w_" + g]) / u[None, :])
    inp["z"] = np.asarray(z, np.float32)
    inp["grad_out"] = go
    return inp


def reference(inputs, h, c, w_i, u_i, b_i, w_f, u_f, b_f, w_c, u_c, b_c, w_o, u_o, b_o, z, grad_out):
    zi, zf, zc, zo = np.split(f64(z), 4, axis=1)
    g = f64(grad_out)
    cf = f64(c)
    i_t = sigmoid(zi)
    f_t = sigmoid(zf)
    c_tilde = np.tanh(zc)
    o_t = sigmoid(zo)
    tc = np.tanh(f_t * cf + i_t * c_tilde)
    dc = g * o_t * (1.0 - tc * tc)
    dzi = dc * c_tilde * i_t * (1.0 - i_t)
    dzf = dc * cf * f_t * (1.0 - f_t)
    dzc = dc * i_t * (1.0 - c_tilde * c_tilde)
    dzo = g * tc * o_t * (1.0 - o_t)
    dz = np.concatenate([dzi, dzf, dzc, dzo], axis=1)
    W = np.concatenate([f64(w_i), f64(w_f), f64(w_c), f64(w_o)], axis=1)
    return mxq(dz, 1, "e5m2") @ mxq(W, 1, "e4m3").T

@@ -1,0 +1,231 @@
+from contextlib import ExitStack
+
+import concourse.mybir as mybir
+from concourse.masks import make_identity
+
+F32 = mybir.dt.float32
+BF16 = mybir.dt.bfloat16
+U32 = mybir.dt.uint32
+U8 = mybir.dt.uint8
+E4M3_X4 = mybir.dt.float8_e4m3fn_x4
+E5M2_X4 = mybir.dt.float8_e5m2_x4
+ACT = mybir.ActivationFunctionType
+ALU = mybir.AluOpType
+
+P = 128
+PACK = 4
+TOKENS, D, U = 2048, 512, 512
+GATES = 4
+N_TILES = TOKENS // P
+LOAD_AHEAD = 3
+
+FLOPS = 2 * TOKENS * D * GATES * U
+BYTES = 4 * TOKENS * GATES * U + 2 * 2 * TOKENS * U + 2 * GATES * D * U + 4 * TOKENS * D
+
+
+def tile_mylstm_v_kernel(
+    tc, inputs, h, c, w_i, u_i, b_i, w_f, u_f, b_f, w_c, u_c, b_c, w_o, u_o, b_o, z, grad_out, out
+):
+    nc = tc.nc
+    weights = [w_i, w_f, w_c, w_o]
+
+    with ExitStack() as pools:
+        const = pools.enter_context(tc.tile_pool(name="const", bufs=1))
+        w_pool = pools.enter_context(tc.tile_pool(name="w_pool", bufs=GATES))
+        loads = pools.enter_context(tc.tile_pool(name="loads", bufs=LOAD_AHEAD + 1))
+        by_token = pools.enter_context(tc.tile_pool(name="by_token", bufs=2))
+        by_unit = pools.enter_context(tc.tile_pool(name="by_unit", bufs=2))
+        results = pools.enter_context(tc.tile_pool(name="results", bufs=3))
+        psum = pools.enter_context(tc.psum_pool(name="psum", bufs=1))
+
+        ident_f32 = const.tile([P, P], F32)
+        make_identity(nc, ident_f32[:])
+        ident_bf16 = const.tile([P, P], BF16)
+        make_identity(nc, ident_bf16[:])
+
+        w_codes = const.tile([P, GATES, D], U32, align_bytes=64)
+        w_scales = const.tile([P, GATES, D], U8, align_bytes=64)
+
+        z_tiles, cg_tiles, w_tiles = {}, {}, {}
+        gate_tiles, product_tiles, bracket_tiles, tanh_tiles, bank_tiles, mx_tiles, acc_tiles = {}, {}, {}, {}, {}, {}, {}
+
+        def load(n):
+            rows = slice(n * P, (n + 1) * P)
+            z_sb = loads.tile([P, GATES * U], F32)
+            nc.sync.dma_start(out=z_sb[:], in_=z[rows, :])
+            cg = loads.tile([P, 2 * U], BF16)
+            nc.sync.dma_start(out=cg[:, 0:U], in_=c[rows, :])
+            nc.sync.dma_start(out=cg[:, U : 2 * U], in_=grad_out[rows, :])
+            z_tiles[n], cg_tiles[n] = z_sb, cg
+
+        def load_weights():
+            for gate in range(GATES):
+                w_rows = w_pool.tile([P, D // P, U], BF16)
+                nc.sync.dma_start(out=w_rows[:], in_=weights[gate].rearrange("(j p) u -> p j u", p=P))
+                w_tiles[gate] = w_rows
+
+        def quantise_weights():
+            for gate in range(GATES):
+                w_grouped = w_pool.tile([P, D, PACK], BF16, align_bytes=64)
+                for half in range(2):
+                    wt = psum.tile([P, PACK, 2 * P], BF16, tag="cell", bufs=2)
+                    for j in range(2):
+                        for t in range(PACK):
+                            nc.tensor.transpose(
+                                wt[:, t, j * P : (j + 1) * P],
+                                w_tiles[gate][:, 2 * half + j, t * P : (t + 1) * P],
+                                ident_bf16[:],
+                            )
+                    nc.scalar.copy(
+                        out=w_grouped[:, half * 2 * P : (half + 1) * 2 * P, :],
+                        in_=wt[:].rearrange("p t d -> p d t"),
+                    )
+                nc.vector.quantize_mx(
+                    out=w_codes[:, gate, :].bitcast(E4M3_X4),
+                    scales=w_scales[:, gate, :],
+                    in_=w_grouped[:].rearrange("p d t -> p (d t)"),
+                )
+
+        def gates(n):
+            z_sb = z_tiles[n]
+            sig = by_token.tile([P, 3 * U], F32, bufs=3)
+            nc.scalar.activation(out=sig[:, 0 : 2 * U], in_=z_sb[:, 0 : 2 * U], func=ACT.Sigmoid)
+            c_tilde = by_token.tile([P, U], F32, bufs=3)
+            nc.scalar.activation(out=c_tilde[:], in_=z_sb[:, 2 * U : 3 * U], func=ACT.Tanh)
+            nc.scalar.activation(out=sig[:, 2 * U : 3 * U], in_=z_sb[:, 3 * U : 4 * U], func=ACT.Sigmoid)
+            c_tilde_sq = by_token.tile([P, U], F32, bufs=3)
+            nc.scalar.activation(out=c_tilde_sq[:], in_=c_tilde[:], func=ACT.Square)
+            gate_tiles[n] = (sig, c_tilde, c_tilde_sq)
+
+        def products(n):
+            sig, c_tilde, c_tilde_sq = gate_tiles[n]
+            cg = cg_tiles[n]
+            prod = by_token.tile([P, 3 * U], F32)
+            nc.vector.tensor_tensor(out=prod[:, 0:U], in0=sig[:, 0:U], in1=c_tilde[:], op=ALU.mult)
+            nc.vector.tensor_tensor(out=prod[:, U : 3 * U], in0=sig[:, U : 3 * U], in1=cg[:], op=ALU.mult)
+            c_new = psum.tile([P, PACK, P], F32, tag="cell", bufs=2)
+            for t in range(PACK):
+                nc.tensor.matmul(
+                    out=c_new[:, t, :], lhsT=prod[:, t * P : (t + 1) * P], rhs=ident_f32[:],
+                    is_transpose=True, start=True, stop=False,
+                )
+                nc.tensor.matmul(
+                    out=c_new[:, t, :], lhsT=prod[:, U + t * P : U + (t + 1) * P], rhs=ident_f32[:],
+                    is_transpose=True, start=False, stop=True,
+                )
+            product_tiles[n] = (prod, c_new)
+
+        def cell_tanh(n):
+            prod, c_new = product_tiles[n]
+            th = by_unit.tile([P, P, PACK], F32)
+            nc.scalar.activation(out=th[:], in_=c_new[:].rearrange("p t b -> p b t"), func=ACT.Tanh)
+            th_sq = by_unit.tile([P, P, PACK], F32)
+            nc.scalar.activation(out=th_sq[:], in_=th[:], func=ACT.Square)
+            tanh_tiles[n] = (th, th_sq)
+
+        def brackets(n):
+            sig, c_tilde, c_tilde_sq = gate_tiles[n]
+            prod, c_new = product_tiles[n]
+            bracket_ifo = by_token.tile([P, 3 * U], F32)
+            nc.vector.scalar_tensor_tensor(
+                out=bracket_ifo[:], in0=sig[:], scalar=1.0, in1=prod[:], op0=ALU.subtract, op1=ALU.mult
+            )
+            bracket_c = by_token.tile([P, U], F32)
+            nc.vector.scalar_tensor_tensor(
+                out=bracket_c[:], in0=c_tilde_sq[:], scalar=1.0, in1=sig[:, 0:U], op0=ALU.subtract, op1=ALU.mult
+            )
+            bracket_tiles[n] = (bracket_ifo, bracket_c)
+
+        def transpose_512(bank, by_token_cols):
+            for t in range(PACK):
+                nc.tensor.transpose(bank[:, t, :], by_token_cols[:, t * P : (t + 1) * P], ident_f32[:])
+
+        def transposes(n):
+            prod, c_new = product_tiles[n]
+            bracket_ifo, bracket_c = bracket_tiles[n]
+            og_t = psum.tile([P, PACK, P], F32)
+            transpose_512(og_t, prod[:, 2 * U : 3 * U])
+            bracket_o_t = psum.tile([P, PACK, P], F32)
+            transpose_512(bracket_o_t, bracket_ifo[:, 2 * U : 3 * U])
+            bracket_i_t = psum.tile([P, PACK, P], F32)
+            transpose_512(bracket_i_t, bracket_ifo[:, 0:U])
+            bracket_f_t = psum.tile([P, PACK, P], F32)
+            transpose_512(bracket_f_t, bracket_ifo[:, U : 2 * U])
+            bracket_c_t = psum.tile([P, PACK, P], F32)
+            transpose_512(bracket_c_t, bracket_c[:])
+            bank_tiles[n] = (og_t, bracket_o_t, bracket_i_t, bracket_f_t, bracket_c_t)
+
+        def word_order(bank):
+            return bank[:].rearrange("p t b -> p b t")
+
+        def gradients(n):
+            th, th_sq = tanh_tiles[n]
+            og_t, bracket_o_t, bracket_i_t, bracket_f_t, bracket_c_t = bank_tiles[n]
+            minus_dc = by_unit.tile([P, P, PACK], F32)
+            nc.vector.scalar_tensor_tensor(
+                out=minus_dc[:], in0=th_sq[:], scalar=1.0, in1=word_order(og_t), op0=ALU.subtract, op1=ALU.mult
+            )
+            dz = by_unit.tile([P, GATES, P, PACK], BF16, align_bytes=64)
+            nc.vector.scalar_tensor_tensor(
+                out=dz[:, 3], in0=word_order(bracket_o_t), scalar=-1.0, in1=th[:], op0=ALU.mult, op1=ALU.mult
+            )
+            nc.vector.tensor_tensor(out=dz[:, 0], in0=word_order(bracket_i_t), in1=minus_dc[:], op=ALU.mult)
+            nc.vector.tensor_tensor(out=dz[:, 1], in0=word_order(bracket_f_t), in1=minus_dc[:], op=ALU.mult)
+            nc.vector.tensor_tensor(out=dz[:, 2], in0=word_order(bracket_c_t), in1=minus_dc[:], op=ALU.mult)
+            dz_codes = results.tile([P, GATES, P], U32, align_bytes=64)
+            dz_scales = results.tile([P, GATES, P], U8, align_bytes=64)
+            nc.vector.quantize_mx(
+                out=dz_codes[:].rearrange("p g b -> p (g b)").bitcast(E5M2_X4),
+                scales=dz_scales[:].rearrange("p g b -> p (g b)"),
+                in_=dz[:].rearrange("p g b t -> p (g b t)"),
+            )
+            mx_tiles[n] = (dz_codes, dz_scales)
+
+        def multiply(n):
+            dz_codes, dz_scales = mx_tiles[n]
+            acc = psum.tile([P, D], F32)
+            for gate in range(GATES):
+                nc.tensor.matmul_mx(
+                    out=acc[:],
+                    lhsT=dz_codes[:, gate, :].bitcast(E5M2_X4),
+                    lhsT_scale=dz_scales[:, gate, :],
+                    rhs=w_codes[:, gate, :].bitcast(E4M3_X4),
+                    rhs_scale=w_scales[:, gate, :],
+                    start=(gate == 0),
+                    stop=(gate == GATES - 1),
+                )
+            acc_tiles[n] = acc
+
+        def store(n):
+            acc = acc_tiles[n]
+            out_rows = results.tile([P, D], F32)
+            nc.scalar.copy(out=out_rows[:], in_=acc[:])
+            nc.scalar.dma_start(out=out[n * P : (n + 1) * P, :], in_=out_rows[:])
+
+        load(0)
+        load(1)
+        load_weights()
+        load(2)
+        gates(0)
+        gates(1)
+        products(0)
+        cell_tanh(0)
+        brackets(0)
+        transposes(0)
+        quantise_weights()
+        for n in range(N_TILES):
+            if n + LOAD_AHEAD < N_TILES:
+                load(n + LOAD_AHEAD)
+            if n >= 1:
+                store(n - 1)
+            if n + 2 < N_TILES:
+                gates(n + 2)
+            if n + 1 < N_TILES:
+                products(n + 1)
+                cell_tanh(n + 1)
+                brackets(n + 1)
+            gradients(n)
+            if n + 1 < N_TILES:
+                transposes(n + 1)
+            multiply(n)
+        store(N_TILES - 1)

@@ -17,7 +17,7 @@ PACK = 4
 TOKENS, D, U = 2048, 512, 512
 GATES = 4
 N_TILES = TOKENS // P
-LOAD_AHEAD = 3
+LOAD_AHEAD = 4
 
 FLOPS = 2 * TOKENS * D * GATES * U
 BYTES = 4 * TOKENS * GATES * U + 2 * 2 * TOKENS * U + 2 * GATES * D * U + 4 * TOKENS * D
@@ -47,7 +47,8 @@ def tile_mylstm_v_kernel(
         w_scales = const.tile([P, GATES, D], U8, align_bytes=64)
 
         z_tiles, cg_tiles, w_tiles = {}, {}, {}
-        gate_tiles, product_tiles, bracket_tiles, tanh_tiles, bank_tiles, mx_tiles, acc_tiles = {}, {}, {}, {}, {}, {}, {}
+        gate_tiles, product_tiles, cell_tiles, bracket_tiles = {}, {}, {}, {}
+        tanh_tiles, bank_tiles, mx_tiles, acc_tiles = {}, {}, {}, {}
 
         def load(n):
             rows = slice(n * P, (n + 1) * P)
@@ -68,7 +69,7 @@ def tile_mylstm_v_kernel(
             for gate in range(GATES):
                 w_grouped = w_pool.tile([P, D, PACK], BF16, align_bytes=64)
                 for half in range(2):
-                    wt = psum.tile([P, PACK, 2 * P], BF16, tag="cell", bufs=2)
+                    wt = psum.tile([P, PACK, 2 * P], BF16, tag="acc", bufs=2)
                     for j in range(2):
                         for t in range(PACK):
                             nc.tensor.transpose(
@@ -88,12 +89,12 @@ def tile_mylstm_v_kernel(
 
         def gates(n):
             z_sb = z_tiles[n]
-            sig = by_token.tile([P, 3 * U], F32, bufs=3)
+            sig = by_token.tile([P, 3 * U], F32, bufs=4)
             nc.scalar.activation(out=sig[:, 0 : 2 * U], in_=z_sb[:, 0 : 2 * U], func=ACT.Sigmoid)
-            c_tilde = by_token.tile([P, U], F32, bufs=3)
+            c_tilde = by_token.tile([P, U], F32, bufs=4)
             nc.scalar.activation(out=c_tilde[:], in_=z_sb[:, 2 * U : 3 * U], func=ACT.Tanh)
             nc.scalar.activation(out=sig[:, 2 * U : 3 * U], in_=z_sb[:, 3 * U : 4 * U], func=ACT.Sigmoid)
-            c_tilde_sq = by_token.tile([P, U], F32, bufs=3)
+            c_tilde_sq = by_token.tile([P, U], F32, bufs=4)
             nc.scalar.activation(out=c_tilde_sq[:], in_=c_tilde[:], func=ACT.Square)
             gate_tiles[n] = (sig, c_tilde, c_tilde_sq)
 
@@ -101,9 +102,13 @@ def tile_mylstm_v_kernel(
             sig, c_tilde, c_tilde_sq = gate_tiles[n]
             cg = cg_tiles[n]
             prod = by_token.tile([P, 3 * U], F32)
-            nc.vector.tensor_tensor(out=prod[:, 0:U], in0=sig[:, 0:U], in1=c_tilde[:], op=ALU.mult)
-            nc.vector.tensor_tensor(out=prod[:, U : 3 * U], in0=sig[:, U : 3 * U], in1=cg[:], op=ALU.mult)
-            c_new = psum.tile([P, PACK, P], F32, tag="cell", bufs=2)
+            nc.gpsimd.tensor_tensor(out=prod[:, 0:U], in0=sig[:, 0:U], in1=c_tilde[:], op=ALU.mult)
+            nc.gpsimd.tensor_tensor(out=prod[:, U : 3 * U], in0=sig[:, U : 3 * U], in1=cg[:], op=ALU.mult)
+            product_tiles[n] = prod
+
+        def cell_sum(n):
+            prod = product_tiles[n]
+            c_new = psum.tile([P, PACK, P], F32)
             for t in range(PACK):
                 nc.tensor.matmul(
                     out=c_new[:, t, :], lhsT=prod[:, t * P : (t + 1) * P], rhs=ident_f32[:],
@@ -113,10 +118,10 @@ def tile_mylstm_v_kernel(
                     out=c_new[:, t, :], lhsT=prod[:, U + t * P : U + (t + 1) * P], rhs=ident_f32[:],
                     is_transpose=True, start=False, stop=True,
                 )
-            product_tiles[n] = (prod, c_new)
+            cell_tiles[n] = c_new
 
         def cell_tanh(n):
-            prod, c_new = product_tiles[n]
+            c_new = cell_tiles[n]
             th = by_unit.tile([P, P, PACK], F32)
             nc.scalar.activation(out=th[:], in_=c_new[:].rearrange("p t b -> p b t"), func=ACT.Tanh)
             th_sq = by_unit.tile([P, P, PACK], F32)
@@ -125,7 +130,7 @@ def tile_mylstm_v_kernel(
 
         def brackets(n):
             sig, c_tilde, c_tilde_sq = gate_tiles[n]
-            prod, c_new = product_tiles[n]
+            prod = product_tiles[n]
             bracket_ifo = by_token.tile([P, 3 * U], F32)
             nc.vector.scalar_tensor_tensor(
                 out=bracket_ifo[:], in0=sig[:], scalar=1.0, in1=prod[:], op0=ALU.subtract, op1=ALU.mult
@@ -141,7 +146,7 @@ def tile_mylstm_v_kernel(
                 nc.tensor.transpose(bank[:, t, :], by_token_cols[:, t * P : (t + 1) * P], ident_f32[:])
 
         def transposes(n):
-            prod, c_new = product_tiles[n]
+            prod = product_tiles[n]
             bracket_ifo, bracket_c = bracket_tiles[n]
             og_t = psum.tile([P, PACK, P], F32)
             transpose_512(og_t, prod[:, 2 * U : 3 * U])
@@ -183,7 +188,7 @@ def tile_mylstm_v_kernel(
 
         def multiply(n):
             dz_codes, dz_scales = mx_tiles[n]
-            acc = psum.tile([P, D], F32)
+            acc = psum.tile([P, D], F32, tag="acc", bufs=2)
             for gate in range(GATES):
                 nc.tensor.matmul_mx(
                     out=acc[:],
@@ -205,27 +210,35 @@ def tile_mylstm_v_kernel(
         load(0)
         load(1)
         load_weights()
-        load(2)
+        for n in range(2, LOAD_AHEAD):
+            load(n)
         gates(0)
-        gates(1)
         products(0)
+        gates(1)
+        cell_sum(0)
+        products(1)
         cell_tanh(0)
         brackets(0)
         transposes(0)
+        cell_sum(1)
+        gates(2)
         quantise_weights()
         for n in range(N_TILES):
             if n + LOAD_AHEAD < N_TILES:
                 load(n + LOAD_AHEAD)
+            if n + 3 < N_TILES:
+                gates(n + 3)
             if n >= 1:
                 store(n - 1)
-            if n + 2 < N_TILES:
-                gates(n + 2)
             if n + 1 < N_TILES:
-                products(n + 1)
                 cell_tanh(n + 1)
                 brackets(n + 1)
+            if n + 2 < N_TILES:
+                products(n + 2)
             gradients(n)
             if n + 1 < N_TILES:
                 transposes(n + 1)
             multiply(n)
+            if n + 2 < N_TILES:
+                cell_sum(n + 2)
         store(N_TILES - 1)

@@ -47,8 +47,8 @@ def tile_mylstm_v_kernel(
         w_scales = const.tile([P, GATES, D], U8, align_bytes=64)
 
         z_tiles, cg_tiles, w_tiles = {}, {}, {}
-        gate_tiles, product_tiles, cell_tiles, bracket_tiles = {}, {}, {}, {}
-        tanh_tiles, bank_tiles, mx_tiles, acc_tiles = {}, {}, {}, {}
+        gate_tiles, product_tiles, og_tiles, cell_tiles, bracket_tiles = {}, {}, {}, {}, {}
+        tanh_tiles, bank_tiles, dz_tiles, mx_tiles, acc_tiles = {}, {}, {}, {}, {}
 
         def load(n):
             rows = slice(n * P, (n + 1) * P)
@@ -66,8 +66,10 @@ def tile_mylstm_v_kernel(
                 w_tiles[gate] = w_rows
 
         def quantise_weights():
+            grouped = []
             for gate in range(GATES):
                 w_grouped = w_pool.tile([P, D, PACK], BF16, align_bytes=64)
+                grouped.append(w_grouped)
                 for half in range(2):
                     wt = psum.tile([P, PACK, 2 * P], BF16, tag="acc", bufs=2)
                     for j in range(2):
@@ -77,14 +79,16 @@ def tile_mylstm_v_kernel(
                                 w_tiles[gate][:, 2 * half + j, t * P : (t + 1) * P],
                                 ident_bf16[:],
                             )
-                    nc.scalar.copy(
-                        out=w_grouped[:, half * 2 * P : (half + 1) * 2 * P, :],
-                        in_=wt[:].rearrange("p t d -> p d t"),
-                    )
+                    d_cols = slice(half * 2 * P, (half + 1) * 2 * P)
+                    if half == 0:
+                        nc.scalar.copy(out=w_grouped[:, d_cols, :], in_=wt[:].rearrange("p t d -> p d t"))
+                    else:
+                        nc.vector.tensor_copy(out=w_grouped[:, d_cols, :], in_=wt[:].rearrange("p t d -> p d t"))
+            for gate in range(GATES):
                 nc.vector.quantize_mx(
                     out=w_codes[:, gate, :].bitcast(E4M3_X4),
                     scales=w_scales[:, gate, :],
-                    in_=w_grouped[:].rearrange("p d t -> p (d t)"),
+                    in_=grouped[gate][:].rearrange("p d t -> p (d t)"),
                 )
 
         def gates(n):
@@ -101,21 +105,28 @@ def tile_mylstm_v_kernel(
         def products(n):
             sig, c_tilde, c_tilde_sq = gate_tiles[n]
             cg = cg_tiles[n]
-            prod = by_token.tile([P, 3 * U], F32)
-            nc.gpsimd.tensor_tensor(out=prod[:, 0:U], in0=sig[:, 0:U], in1=c_tilde[:], op=ALU.mult)
-            nc.gpsimd.tensor_tensor(out=prod[:, U : 3 * U], in0=sig[:, U : 3 * U], in1=cg[:], op=ALU.mult)
-            product_tiles[n] = prod
+            prod_ab = by_token.tile([P, 2 * U], F32, bufs=1)
+            nc.gpsimd.tensor_tensor(out=prod_ab[:, 0:U], in0=sig[:, 0:U], in1=c_tilde[:], op=ALU.mult)
+            nc.gpsimd.tensor_tensor(out=prod_ab[:, U : 2 * U], in0=sig[:, U : 2 * U], in1=cg[:, 0:U], op=ALU.mult)
+            product_tiles[n] = prod_ab
+
+        def output_product(n):
+            sig, c_tilde, c_tilde_sq = gate_tiles[n]
+            cg = cg_tiles[n]
+            prod_og = by_token.tile([P, U], F32)
+            nc.vector.tensor_tensor(out=prod_og[:], in0=sig[:, 2 * U : 3 * U], in1=cg[:, U : 2 * U], op=ALU.mult)
+            og_tiles[n] = prod_og
 
         def cell_sum(n):
-            prod = product_tiles[n]
+            prod_ab = product_tiles[n]
             c_new = psum.tile([P, PACK, P], F32)
             for t in range(PACK):
                 nc.tensor.matmul(
-                    out=c_new[:, t, :], lhsT=prod[:, t * P : (t + 1) * P], rhs=ident_f32[:],
+                    out=c_new[:, t, :], lhsT=prod_ab[:, t * P : (t + 1) * P], rhs=ident_f32[:],
                     is_transpose=True, start=True, stop=False,
                 )
                 nc.tensor.matmul(
-                    out=c_new[:, t, :], lhsT=prod[:, U + t * P : U + (t + 1) * P], rhs=ident_f32[:],
+                    out=c_new[:, t, :], lhsT=prod_ab[:, U + t * P : U + (t + 1) * P], rhs=ident_f32[:],
                     is_transpose=True, start=False, stop=True,
                 )
             cell_tiles[n] = c_new
@@ -130,32 +141,36 @@ def tile_mylstm_v_kernel(
 
         def brackets(n):
             sig, c_tilde, c_tilde_sq = gate_tiles[n]
-            prod = product_tiles[n]
-            bracket_ifo = by_token.tile([P, 3 * U], F32)
-            nc.vector.scalar_tensor_tensor(
-                out=bracket_ifo[:], in0=sig[:], scalar=1.0, in1=prod[:], op0=ALU.subtract, op1=ALU.mult
-            )
             bracket_c = by_token.tile([P, U], F32)
             nc.vector.scalar_tensor_tensor(
                 out=bracket_c[:], in0=c_tilde_sq[:], scalar=1.0, in1=sig[:, 0:U], op0=ALU.subtract, op1=ALU.mult
             )
-            bracket_tiles[n] = (bracket_ifo, bracket_c)
+            bracket_o = by_token.tile([P, U], F32)
+            nc.vector.scalar_tensor_tensor(
+                out=bracket_o[:], in0=sig[:, 2 * U : 3 * U], scalar=1.0, in1=og_tiles[n][:],
+                op0=ALU.subtract, op1=ALU.mult,
+            )
+            bracket_if = by_token.tile([P, 2 * U], F32)
+            nc.vector.scalar_tensor_tensor(
+                out=bracket_if[:], in0=sig[:, 0 : 2 * U], scalar=1.0, in1=product_tiles[n][:],
+                op0=ALU.subtract, op1=ALU.mult,
+            )
+            bracket_tiles[n] = (bracket_if, bracket_o, bracket_c)
 
         def transpose_512(bank, by_token_cols):
             for t in range(PACK):
                 nc.tensor.transpose(bank[:, t, :], by_token_cols[:, t * P : (t + 1) * P], ident_f32[:])
 
         def transposes(n):
-            prod = product_tiles[n]
-            bracket_ifo, bracket_c = bracket_tiles[n]
+            bracket_if, bracket_o, bracket_c = bracket_tiles[n]
             og_t = psum.tile([P, PACK, P], F32)
-            transpose_512(og_t, prod[:, 2 * U : 3 * U])
+            transpose_512(og_t, og_tiles[n][:])
             bracket_o_t = psum.tile([P, PACK, P], F32)
-            transpose_512(bracket_o_t, bracket_ifo[:, 2 * U : 3 * U])
+            transpose_512(bracket_o_t, bracket_o[:])
             bracket_i_t = psum.tile([P, PACK, P], F32)
-            transpose_512(bracket_i_t, bracket_ifo[:, 0:U])
+            transpose_512(bracket_i_t, bracket_if[:, 0:U])
             bracket_f_t = psum.tile([P, PACK, P], F32)
-            transpose_512(bracket_f_t, bracket_ifo[:, U : 2 * U])
+            transpose_512(bracket_f_t, bracket_if[:, U : 2 * U])
             bracket_c_t = psum.tile([P, PACK, P], F32)
             transpose_512(bracket_c_t, bracket_c[:])
             bank_tiles[n] = (og_t, bracket_o_t, bracket_i_t, bracket_f_t, bracket_c_t)
@@ -177,6 +192,10 @@ def tile_mylstm_v_kernel(
             nc.vector.tensor_tensor(out=dz[:, 0], in0=word_order(bracket_i_t), in1=minus_dc[:], op=ALU.mult)
             nc.vector.tensor_tensor(out=dz[:, 1], in0=word_order(bracket_f_t), in1=minus_dc[:], op=ALU.mult)
             nc.vector.tensor_tensor(out=dz[:, 2], in0=word_order(bracket_c_t), in1=minus_dc[:], op=ALU.mult)
+            dz_tiles[n] = dz
+
+        def quantise(n):
+            dz = dz_tiles[n]
             dz_codes = results.tile([P, GATES, P], U32, align_bytes=64)
             dz_scales = results.tile([P, GATES, P], U8, align_bytes=64)
             nc.vector.quantize_mx(
@@ -207,38 +226,45 @@ def tile_mylstm_v_kernel(
             nc.scalar.copy(out=out_rows[:], in_=acc[:])
             nc.scalar.dma_start(out=out[n * P : (n + 1) * P, :], in_=out_rows[:])
 
-        load(0)
-        load(1)
-        load_weights()
-        for n in range(2, LOAD_AHEAD):
-            load(n)
-        gates(0)
-        products(0)
-        gates(1)
-        cell_sum(0)
-        products(1)
-        cell_tanh(0)
-        brackets(0)
-        transposes(0)
-        cell_sum(1)
-        gates(2)
-        quantise_weights()
-        for n in range(N_TILES):
-            if n + LOAD_AHEAD < N_TILES:
-                load(n + LOAD_AHEAD)
-            if n + 3 < N_TILES:
-                gates(n + 3)
-            if n >= 1:
-                store(n - 1)
-            if n + 1 < N_TILES:
-                cell_tanh(n + 1)
-                brackets(n + 1)
-            if n + 2 < N_TILES:
-                products(n + 2)
-            gradients(n)
-            if n + 1 < N_TILES:
-                transposes(n + 1)
-            multiply(n)
-            if n + 2 < N_TILES:
-                cell_sum(n + 2)
-        store(N_TILES - 1)
+        with tc.manual_schedule():
+            load_weights()
+            for n in range(LOAD_AHEAD):
+                load(n)
+            quantise_weights()
+            gates(0)
+            products(0)
+            output_product(0)
+            cell_sum(0)
+            gates(1)
+            cell_tanh(0)
+            brackets(0)
+            transposes(0)
+            products(1)
+            output_product(1)
+            cell_sum(1)
+            gates(2)
+            for n in range(N_TILES):
+                if n + LOAD_AHEAD < N_TILES:
+                    load(n + LOAD_AHEAD)
+                if n >= 1:
+                    multiply(n - 1)
+                if n + 3 < N_TILES:
+                    gates(n + 3)
+                if n + 1 < N_TILES:
+                    cell_tanh(n + 1)
+                if n >= 1:
+                    store(n - 1)
+                if n + 1 < N_TILES:
+                    brackets(n + 1)
+                if n + 2 < N_TILES:
+                    products(n + 2)
+                gradients(n)
+                if n + 2 < N_TILES:
+                    output_product(n + 2)
+                quantise(n)
+                if n + 1 < N_TILES:
+                    transposes(n + 1)
+                if n + 2 < N_TILES:
+                    cell_sum(n + 2)
+            multiply(N_TILES - 1)
+            store(N_TILES - 1)

@@ -18,6 +18,8 @@ TOKENS, D, U = 2048, 512, 512
 GATES = 4
 N_TILES = TOKENS // P
 LOAD_AHEAD = 4
+FIRST_MX_ROUND = GATES + 1
+MX_TILES_A_ROUND = 2
 
 FLOPS = 2 * TOKENS * D * GATES * U
 BYTES = 4 * TOKENS * GATES * U + 2 * 2 * TOKENS * U + 2 * GATES * D * U + 4 * TOKENS * D
@@ -35,6 +37,7 @@ def tile_mylstm_v_kernel(
         loads = pools.enter_context(tc.tile_pool(name="loads", bufs=LOAD_AHEAD + 1))
         by_token = pools.enter_context(tc.tile_pool(name="by_token", bufs=2))
         by_unit = pools.enter_context(tc.tile_pool(name="by_unit", bufs=2))
+        quantised = pools.enter_context(tc.tile_pool(name="quantised", bufs=FIRST_MX_ROUND + 2))
         results = pools.enter_context(tc.tile_pool(name="results", bufs=3))
         psum = pools.enter_context(tc.psum_pool(name="psum", bufs=1))
 
@@ -46,16 +49,17 @@ def tile_mylstm_v_kernel(
         w_codes = const.tile([P, GATES, D], U32, align_bytes=64)
         w_scales = const.tile([P, GATES, D], U8, align_bytes=64)
 
-        z_tiles, cg_tiles, w_tiles = {}, {}, {}
+        z_tiles, cg_tiles, w_tiles, wt_tiles, grouped_tiles = {}, {}, {}, {}, {}
         gate_tiles, product_tiles, og_tiles, cell_tiles, bracket_tiles = {}, {}, {}, {}, {}
         tanh_tiles, bank_tiles, dz_tiles, mx_tiles, acc_tiles = {}, {}, {}, {}, {}
 
         def load(n):
             rows = slice(n * P, (n + 1) * P)
             z_sb = loads.tile([P, GATES * U], F32)
-            nc.sync.dma_start(out=z_sb[:], in_=z[rows, :])
             cg = loads.tile([P, 2 * U], BF16)
+            nc.sync.dma_start(out=z_sb[:, 0 : 2 * U], in_=z[rows, 0 : 2 * U])
             nc.sync.dma_start(out=cg[:, 0:U], in_=c[rows, :])
+            nc.sync.dma_start(out=z_sb[:, 2 * U : 4 * U], in_=z[rows, 2 * U : 4 * U])
             nc.sync.dma_start(out=cg[:, U : 2 * U], in_=grad_out[rows, :])
             z_tiles[n], cg_tiles[n] = z_sb, cg
 
@@ -65,31 +69,33 @@ def tile_mylstm_v_kernel(
                 nc.sync.dma_start(out=w_rows[:], in_=weights[gate].rearrange("(j p) u -> p j u", p=P))
                 w_tiles[gate] = w_rows
 
-        def quantise_weights():
-            grouped = []
-            for gate in range(GATES):
-                w_grouped = w_pool.tile([P, D, PACK], BF16, align_bytes=64)
-                grouped.append(w_grouped)
-                for half in range(2):
-                    wt = psum.tile([P, PACK, 2 * P], BF16, tag="acc", bufs=2)
-                    for j in range(2):
-                        for t in range(PACK):
-                            nc.tensor.transpose(
-                                wt[:, t, j * P : (j + 1) * P],
-                                w_tiles[gate][:, 2 * half + j, t * P : (t + 1) * P],
-                                ident_bf16[:],
-                            )
-                    d_cols = slice(half * 2 * P, (half + 1) * 2 * P)
-                    if half == 0:
-                        nc.scalar.copy(out=w_grouped[:, d_cols, :], in_=wt[:].rearrange("p t d -> p d t"))
-                    else:
-                        nc.vector.tensor_copy(out=w_grouped[:, d_cols, :], in_=wt[:].rearrange("p t d -> p d t"))
-            for gate in range(GATES):
-                nc.vector.quantize_mx(
-                    out=w_codes[:, gate, :].bitcast(E4M3_X4),
-                    scales=w_scales[:, gate, :],
-                    in_=grouped[gate][:].rearrange("p d t -> p (d t)"),
+        def transpose_weights(gate):
+            w_grouped = w_pool.tile([P, D, PACK], BF16, align_bytes=64)
+            for half in range(2):
+                wt = psum.tile([P, PACK, 2 * P], BF16, tag="acc", bufs=2)
+                for j in range(2):
+                    for t in range(PACK):
+                        nc.tensor.transpose(
+                            wt[:, t, j * P : (j + 1) * P],
+                            w_tiles[gate][:, 2 * half + j, t * P : (t + 1) * P],
+                            ident_bf16[:],
+                        )
+                wt_tiles[(gate, half)] = wt
+            grouped_tiles[gate] = w_grouped
+
+        def group_weights(gate):
+            for half in range(2):
+                nc.scalar.copy(
+                    out=grouped_tiles[gate][:, half * 2 * P : (half + 1) * 2 * P, :],
+                    in_=wt_tiles[(gate, half)][:].rearrange("p t d -> p d t"),
                 )
+
+        def quantise_weights(gate):
+            nc.vector.quantize_mx(
+                out=w_codes[:, gate, :].bitcast(E4M3_X4),
+                scales=w_scales[:, gate, :],
+                in_=grouped_tiles[gate][:].rearrange("p d t -> p (d t)"),
+            )
 
         def gates(n):
             z_sb = z_tiles[n]
@@ -102,12 +108,12 @@ def tile_mylstm_v_kernel(
             nc.scalar.activation(out=c_tilde_sq[:], in_=c_tilde[:], func=ACT.Square)
             gate_tiles[n] = (sig, c_tilde, c_tilde_sq)
 
-        def products(n):
+        def products(n, engine):
             sig, c_tilde, c_tilde_sq = gate_tiles[n]
             cg = cg_tiles[n]
             prod_ab = by_token.tile([P, 2 * U], F32, bufs=1)
-            nc.gpsimd.tensor_tensor(out=prod_ab[:, 0:U], in0=sig[:, 0:U], in1=c_tilde[:], op=ALU.mult)
-            nc.gpsimd.tensor_tensor(out=prod_ab[:, U : 2 * U], in0=sig[:, U : 2 * U], in1=cg[:, 0:U], op=ALU.mult)
+            engine.tensor_tensor(out=prod_ab[:, U : 2 * U], in0=sig[:, U : 2 * U], in1=cg[:, 0:U], op=ALU.mult)
+            engine.tensor_tensor(out=prod_ab[:, 0:U], in0=sig[:, 0:U], in1=c_tilde[:], op=ALU.mult)
             product_tiles[n] = prod_ab
 
         def output_product(n):
@@ -196,8 +202,8 @@ def tile_mylstm_v_kernel(
 
         def quantise(n):
             dz = dz_tiles[n]
-            dz_codes = results.tile([P, GATES, P], U32, align_bytes=64)
-            dz_scales = results.tile([P, GATES, P], U8, align_bytes=64)
+            dz_codes = quantised.tile([P, GATES, P], U32, align_bytes=64)
+            dz_scales = quantised.tile([P, GATES, P], U8, align_bytes=64)
             nc.vector.quantize_mx(
                 out=dz_codes[:].rearrange("p g b -> p (g b)").bitcast(E5M2_X4),
                 scales=dz_scales[:].rearrange("p g b -> p (g b)"),
@@ -227,41 +233,50 @@ def tile_mylstm_v_kernel(
             nc.scalar.dma_start(out=out[n * P : (n + 1) * P, :], in_=out_rows[:])
 
         with tc.manual_schedule():
-            load_weights()
             for n in range(LOAD_AHEAD):
                 load(n)
-            quantise_weights()
+            load_weights()
             gates(0)
-            products(0)
+            products(0, nc.vector)
             output_product(0)
             cell_sum(0)
             gates(1)
             cell_tanh(0)
             brackets(0)
             transposes(0)
-            products(1)
+            products(1, nc.vector)
             output_product(1)
             cell_sum(1)
             gates(2)
+            multiplied = 0
             for n in range(N_TILES):
                 if n + LOAD_AHEAD < N_TILES:
                     load(n + LOAD_AHEAD)
-                if n >= 1:
-                    multiply(n - 1)
+                if n < GATES:
+                    transpose_weights(n)
+                first_of_round = multiplied
+                if n >= FIRST_MX_ROUND:
+                    multiplied = min(n, first_of_round + MX_TILES_A_ROUND)
+                for m in range(first_of_round, multiplied):
+                    multiply(m)
                 if n + 3 < N_TILES:
                     gates(n + 3)
                 if n + 1 < N_TILES:
                     cell_tanh(n + 1)
-                if n >= 1:
-                    store(n - 1)
+                if n < GATES:
+                    group_weights(n)
+                for m in range(first_of_round, multiplied):
+                    store(m)
                 if n + 1 < N_TILES:
                     brackets(n + 1)
                 if n + 2 < N_TILES:
-                    products(n + 2)
+                    products(n + 2, nc.gpsimd)
                 gradients(n)
                 if n + 2 < N_TILES:
                     output_product(n + 2)
                 quantise(n)
+                if 1 <= n <= GATES:
+                    quantise_weights(n - 1)
                 if n + 1 < N_TILES:
                     transposes(n + 1)
                 if n + 2 < N_TILES:

@@ -254,32 +254,33 @@ def tile_mylstm_v_kernel(
                     load(n + LOAD_AHEAD)
                 if n < GATES:
                     transpose_weights(n)
-                first_of_round = multiplied
-                if n >= FIRST_MX_ROUND:
-                    multiplied = min(n, first_of_round + MX_TILES_A_ROUND)
-                for m in range(first_of_round, multiplied):
-                    multiply(m)
                 if n + 3 < N_TILES:
                     gates(n + 3)
                 if n + 1 < N_TILES:
                     cell_tanh(n + 1)
                 if n < GATES:
                     group_weights(n)
-                for m in range(first_of_round, multiplied):
-                    store(m)
                 if n + 1 < N_TILES:
                     brackets(n + 1)
+                if n >= 1:
+                    quantise(n - 1)
+                first_of_round = multiplied
+                if n >= FIRST_MX_ROUND:
+                    multiplied = min(n, first_of_round + MX_TILES_A_ROUND)
+                for m in range(first_of_round, multiplied):
+                    multiply(m)
+                    store(m)
                 if n + 2 < N_TILES:
                     products(n + 2, nc.gpsimd)
                 gradients(n)
                 if n + 2 < N_TILES:
                     output_product(n + 2)
-                quantise(n)
                 if 1 <= n <= GATES:
                     quantise_weights(n - 1)
                 if n + 1 < N_TILES:
                     transposes(n + 1)
                 if n + 2 < N_TILES:
                     cell_sum(n + 2)
+            quantise(N_TILES - 1)
             multiply(N_TILES - 1)
             store(N_TILES - 1)

@@ -18,6 +18,7 @@ TOKENS, D, U = 2048, 512, 512
 GATES = 4
 N_TILES = TOKENS // P
 LOAD_AHEAD = 4
+GATES_AHEAD = 3
 FIRST_MX_ROUND = GATES + 1
 MX_TILES_A_ROUND = 2
 
@@ -38,7 +39,7 @@ def tile_mylstm_v_kernel(
         by_token = pools.enter_context(tc.tile_pool(name="by_token", bufs=2))
         by_unit = pools.enter_context(tc.tile_pool(name="by_unit", bufs=2))
         quantised = pools.enter_context(tc.tile_pool(name="quantised", bufs=FIRST_MX_ROUND + 2))
-        results = pools.enter_context(tc.tile_pool(name="results", bufs=3))
+        results = pools.enter_context(tc.tile_pool(name="results", bufs=MX_TILES_A_ROUND + 1))
         psum = pools.enter_context(tc.psum_pool(name="psum", bufs=1))
 
         ident_f32 = const.tile([P, P], F32)
@@ -49,9 +50,9 @@ def tile_mylstm_v_kernel(
         w_codes = const.tile([P, GATES, D], U32, align_bytes=64)
         w_scales = const.tile([P, GATES, D], U8, align_bytes=64)
 
-        z_tiles, cg_tiles, w_tiles, wt_tiles, grouped_tiles = {}, {}, {}, {}, {}
-        gate_tiles, product_tiles, og_tiles, cell_tiles, bracket_tiles = {}, {}, {}, {}, {}
-        tanh_tiles, bank_tiles, dz_tiles, mx_tiles, acc_tiles = {}, {}, {}, {}, {}
+        z_of, cg_of, sig_of, c_tilde_of, c_tilde_sq_of, prod_a_of, prod_bog_of = {}, {}, {}, {}, {}, {}, {}
+        c_new_of, th_of, th_sq_of, brackets_of, banks_of, dz_of, mx_of, acc_of = {}, {}, {}, {}, {}, {}, {}, {}
+        w_rows_of, wt_of, w_grouped_of = {}, {}, {}
 
         def load(n):
             rows = slice(n * P, (n + 1) * P)
@@ -61,158 +62,155 @@ def tile_mylstm_v_kernel(
             nc.sync.dma_start(out=cg[:, 0:U], in_=c[rows, :])
             nc.sync.dma_start(out=z_sb[:, 2 * U : 4 * U], in_=z[rows, 2 * U : 4 * U])
             nc.sync.dma_start(out=cg[:, U : 2 * U], in_=grad_out[rows, :])
-            z_tiles[n], cg_tiles[n] = z_sb, cg
+            z_of[n], cg_of[n] = z_sb, cg
 
         def load_weights():
             for gate in range(GATES):
                 w_rows = w_pool.tile([P, D // P, U], BF16)
                 nc.sync.dma_start(out=w_rows[:], in_=weights[gate].rearrange("(j p) u -> p j u", p=P))
-                w_tiles[gate] = w_rows
+                w_rows_of[gate] = w_rows
 
         def transpose_weights(gate):
-            w_grouped = w_pool.tile([P, D, PACK], BF16, align_bytes=64)
             for half in range(2):
                 wt = psum.tile([P, PACK, 2 * P], BF16, tag="acc", bufs=2)
                 for j in range(2):
                     for t in range(PACK):
                         nc.tensor.transpose(
                             wt[:, t, j * P : (j + 1) * P],
-                            w_tiles[gate][:, 2 * half + j, t * P : (t + 1) * P],
+                            w_rows_of[gate][:, 2 * half + j, t * P : (t + 1) * P],
                             ident_bf16[:],
                         )
-                wt_tiles[(gate, half)] = wt
-            grouped_tiles[gate] = w_grouped
+                wt_of[(gate, half)] = wt
 
         def group_weights(gate):
+            w_grouped = w_pool.tile([P, D, PACK], BF16, align_bytes=64)
             for half in range(2):
                 nc.scalar.copy(
-                    out=grouped_tiles[gate][:, half * 2 * P : (half + 1) * 2 * P, :],
-                    in_=wt_tiles[(gate, half)][:].rearrange("p t d -> p d t"),
+                    out=w_grouped[:, half * 2 * P : (half + 1) * 2 * P, :],
+                    in_=wt_of[(gate, half)][:].rearrange("p t d -> p d t"),
                 )
+            w_grouped_of[gate] = w_grouped
 
         def quantise_weights(gate):
             nc.vector.quantize_mx(
                 out=w_codes[:, gate, :].bitcast(E4M3_X4),
                 scales=w_scales[:, gate, :],
-                in_=grouped_tiles[gate][:].rearrange("p d t -> p (d t)"),
+                in_=w_grouped_of[gate][:].rearrange("p d t -> p (d t)"),
             )
 
         def gates(n):
-            z_sb = z_tiles[n]
-            sig = by_token.tile([P, 3 * U], F32, bufs=4)
+            z_sb = z_of[n]
+            sig = by_token.tile([P, 3 * U], F32, bufs=GATES_AHEAD + 1)
             nc.scalar.activation(out=sig[:, 0 : 2 * U], in_=z_sb[:, 0 : 2 * U], func=ACT.Sigmoid)
-            c_tilde = by_token.tile([P, U], F32, bufs=4)
+            c_tilde = by_token.tile([P, U], F32, bufs=GATES_AHEAD + 1)
             nc.scalar.activation(out=c_tilde[:], in_=z_sb[:, 2 * U : 3 * U], func=ACT.Tanh)
             nc.scalar.activation(out=sig[:, 2 * U : 3 * U], in_=z_sb[:, 3 * U : 4 * U], func=ACT.Sigmoid)
-            c_tilde_sq = by_token.tile([P, U], F32, bufs=4)
+            c_tilde_sq = by_token.tile([P, U], F32, bufs=GATES_AHEAD + 1)
             nc.scalar.activation(out=c_tilde_sq[:], in_=c_tilde[:], func=ACT.Square)
-            gate_tiles[n] = (sig, c_tilde, c_tilde_sq)
+            sig_of[n], c_tilde_of[n], c_tilde_sq_of[n] = sig, c_tilde, c_tilde_sq
 
         def products(n, engine):
-            sig, c_tilde, c_tilde_sq = gate_tiles[n]
-            cg = cg_tiles[n]
-            prod_ab = by_token.tile([P, 2 * U], F32, bufs=1)
-            engine.tensor_tensor(out=prod_ab[:, U : 2 * U], in0=sig[:, U : 2 * U], in1=cg[:, 0:U], op=ALU.mult)
-            engine.tensor_tensor(out=prod_ab[:, 0:U], in0=sig[:, 0:U], in1=c_tilde[:], op=ALU.mult)
-            product_tiles[n] = prod_ab
-
-        def output_product(n):
-            sig, c_tilde, c_tilde_sq = gate_tiles[n]
-            cg = cg_tiles[n]
-            prod_og = by_token.tile([P, U], F32)
-            nc.vector.tensor_tensor(out=prod_og[:], in0=sig[:, 2 * U : 3 * U], in1=cg[:, U : 2 * U], op=ALU.mult)
-            og_tiles[n] = prod_og
+            sig = sig_of[n]
+            prod_a = by_token.tile([P, U], F32, bufs=1)
+            engine.tensor_tensor(out=prod_a[:], in0=sig[:, 0:U], in1=c_tilde_of[n][:], op=ALU.mult)
+            prod_bog = by_token.tile([P, 2 * U], F32)
+            engine.tensor_tensor(out=prod_bog[:], in0=sig[:, U : 3 * U], in1=cg_of[n][:], op=ALU.mult)
+            prod_a_of[n], prod_bog_of[n] = prod_a, prod_bog
 
         def cell_sum(n):
-            prod_ab = product_tiles[n]
             c_new = psum.tile([P, PACK, P], F32)
             for t in range(PACK):
+                units = slice(t * P, (t + 1) * P)
                 nc.tensor.matmul(
-                    out=c_new[:, t, :], lhsT=prod_ab[:, t * P : (t + 1) * P], rhs=ident_f32[:],
+                    out=c_new[:, t, :], lhsT=prod_a_of[n][:, units], rhs=ident_f32[:],
                     is_transpose=True, start=True, stop=False,
                 )
                 nc.tensor.matmul(
-                    out=c_new[:, t, :], lhsT=prod_ab[:, U + t * P : U + (t + 1) * P], rhs=ident_f32[:],
+                    out=c_new[:, t, :], lhsT=prod_bog_of[n][:, units], rhs=ident_f32[:],
                     is_transpose=True, start=False, stop=True,
                 )
-            cell_tiles[n] = c_new
+            c_new_of[n] = c_new
+
+        def word_order(bank):
+            return bank[:].rearrange("p t b -> p b t")
 
         def cell_tanh(n):
-            c_new = cell_tiles[n]
             th = by_unit.tile([P, P, PACK], F32)
-            nc.scalar.activation(out=th[:], in_=c_new[:].rearrange("p t b -> p b t"), func=ACT.Tanh)
+            nc.scalar.activation(out=th[:], in_=word_order(c_new_of[n]), func=ACT.Tanh)
             th_sq = by_unit.tile([P, P, PACK], F32)
             nc.scalar.activation(out=th_sq[:], in_=th[:], func=ACT.Square)
-            tanh_tiles[n] = (th, th_sq)
+            th_of[n], th_sq_of[n] = th, th_sq
 
         def brackets(n):
-            sig, c_tilde, c_tilde_sq = gate_tiles[n]
+            sig = sig_of[n]
             bracket_c = by_token.tile([P, U], F32)
             nc.vector.scalar_tensor_tensor(
-                out=bracket_c[:], in0=c_tilde_sq[:], scalar=1.0, in1=sig[:, 0:U], op0=ALU.subtract, op1=ALU.mult
-            )
-            bracket_o = by_token.tile([P, U], F32)
-            nc.vector.scalar_tensor_tensor(
-                out=bracket_o[:], in0=sig[:, 2 * U : 3 * U], scalar=1.0, in1=og_tiles[n][:],
+                out=bracket_c[:], in0=c_tilde_sq_of[n][:], scalar=1.0, in1=sig[:, 0:U],
                 op0=ALU.subtract, op1=ALU.mult,
             )
-            bracket_if = by_token.tile([P, 2 * U], F32)
+            bracket_f = by_token.tile([P, U], F32)
             nc.vector.scalar_tensor_tensor(
-                out=bracket_if[:], in0=sig[:, 0 : 2 * U], scalar=1.0, in1=product_tiles[n][:],
+                out=bracket_f[:], in0=sig[:, U : 2 * U], scalar=1.0, in1=prod_bog_of[n][:, 0:U],
                 op0=ALU.subtract, op1=ALU.mult,
             )
-            bracket_tiles[n] = (bracket_if, bracket_o, bracket_c)
+            bracket_i = by_token.tile([P, U], F32)
+            nc.vector.scalar_tensor_tensor(
+                out=bracket_i[:], in0=sig[:, 0:U], scalar=1.0, in1=prod_a_of[n][:],
+                op0=ALU.subtract, op1=ALU.mult,
+            )
+            brackets_of[n] = (bracket_i, bracket_f, bracket_c)
 
         def transpose_512(bank, by_token_cols):
             for t in range(PACK):
                 nc.tensor.transpose(bank[:, t, :], by_token_cols[:, t * P : (t + 1) * P], ident_f32[:])
 
         def transposes(n):
-            bracket_if, bracket_o, bracket_c = bracket_tiles[n]
-            og_t = psum.tile([P, PACK, P], F32)
-            transpose_512(og_t, og_tiles[n][:])
-            bracket_o_t = psum.tile([P, PACK, P], F32)
-            transpose_512(bracket_o_t, bracket_o[:])
+            bracket_i, bracket_f, bracket_c = brackets_of[n]
+            o_t = psum.tile([P, PACK, P], F32)
+            transpose_512(o_t, sig_of[n][:, 2 * U : 3 * U])
             bracket_i_t = psum.tile([P, PACK, P], F32)
-            transpose_512(bracket_i_t, bracket_if[:, 0:U])
+            transpose_512(bracket_i_t, bracket_i[:])
+            og_t = psum.tile([P, PACK, P], F32)
+            transpose_512(og_t, prod_bog_of[n][:, U : 2 * U])
             bracket_f_t = psum.tile([P, PACK, P], F32)
-            transpose_512(bracket_f_t, bracket_if[:, U : 2 * U])
+            transpose_512(bracket_f_t, bracket_f[:])
             bracket_c_t = psum.tile([P, PACK, P], F32)
             transpose_512(bracket_c_t, bracket_c[:])
-            bank_tiles[n] = (og_t, bracket_o_t, bracket_i_t, bracket_f_t, bracket_c_t)
-
-        def word_order(bank):
-            return bank[:].rearrange("p t b -> p b t")
+            banks_of[n] = (o_t, bracket_i_t, og_t, bracket_f_t, bracket_c_t)
 
         def gradients(n):
-            th, th_sq = tanh_tiles[n]
-            og_t, bracket_o_t, bracket_i_t, bracket_f_t, bracket_c_t = bank_tiles[n]
+            o_t, bracket_i_t, og_t, bracket_f_t, bracket_c_t = banks_of[n]
+            th = th_of[n]
             minus_dc = by_unit.tile([P, P, PACK], F32)
             nc.vector.scalar_tensor_tensor(
-                out=minus_dc[:], in0=th_sq[:], scalar=1.0, in1=word_order(og_t), op0=ALU.subtract, op1=ALU.mult
+                out=minus_dc[:], in0=th_sq_of[n][:], scalar=1.0, in1=word_order(og_t),
+                op0=ALU.subtract, op1=ALU.mult,
+            )
+            o_th = by_unit.tile([P, P, PACK], F32)
+            nc.vector.scalar_tensor_tensor(
+                out=o_th[:], in0=word_order(o_t), scalar=1.0, in1=th[:], op0=ALU.subtract, op1=ALU.mult
             )
             dz = by_unit.tile([P, GATES, P, PACK], BF16, align_bytes=64)
-            nc.vector.scalar_tensor_tensor(
-                out=dz[:, 3], in0=word_order(bracket_o_t), scalar=-1.0, in1=th[:], op0=ALU.mult, op1=ALU.mult
-            )
             nc.vector.tensor_tensor(out=dz[:, 0], in0=word_order(bracket_i_t), in1=minus_dc[:], op=ALU.mult)
+            nc.vector.scalar_tensor_tensor(
+                out=dz[:, 3], in0=word_order(og_t), scalar=-1.0, in1=o_th[:], op0=ALU.mult, op1=ALU.mult
+            )
             nc.vector.tensor_tensor(out=dz[:, 1], in0=word_order(bracket_f_t), in1=minus_dc[:], op=ALU.mult)
             nc.vector.tensor_tensor(out=dz[:, 2], in0=word_order(bracket_c_t), in1=minus_dc[:], op=ALU.mult)
-            dz_tiles[n] = dz
+            dz_of[n] = dz
 
         def quantise(n):
-            dz = dz_tiles[n]
             dz_codes = quantised.tile([P, GATES, P], U32, align_bytes=64)
             dz_scales = quantised.tile([P, GATES, P], U8, align_bytes=64)
             nc.vector.quantize_mx(
                 out=dz_codes[:].rearrange("p g b -> p (g b)").bitcast(E5M2_X4),
                 scales=dz_scales[:].rearrange("p g b -> p (g b)"),
-                in_=dz[:].rearrange("p g b t -> p (g b t)"),
+                in_=dz_of[n][:].rearrange("p g b t -> p (g b t)"),
             )
-            mx_tiles[n] = (dz_codes, dz_scales)
+            mx_of[n] = (dz_codes, dz_scales)
 
         def multiply(n):
-            dz_codes, dz_scales = mx_tiles[n]
+            dz_codes, dz_scales = mx_of[n]
             acc = psum.tile([P, D], F32, tag="acc", bufs=2)
             for gate in range(GATES):
                 nc.tensor.matmul_mx(
@@ -224,12 +222,11 @@ def tile_mylstm_v_kernel(
                     start=(gate == 0),
                     stop=(gate == GATES - 1),
                 )
-            acc_tiles[n] = acc
+            acc_of[n] = acc
 
         def store(n):
-            acc = acc_tiles[n]
             out_rows = results.tile([P, D], F32)
-            nc.scalar.copy(out=out_rows[:], in_=acc[:])
+            nc.scalar.copy(out=out_rows[:], in_=acc_of[n][:])
             nc.scalar.dma_start(out=out[n * P : (n + 1) * P, :], in_=out_rows[:])
 
         with tc.manual_schedule():
@@ -238,14 +235,12 @@ def tile_mylstm_v_kernel(
             load_weights()
             gates(0)
             products(0, nc.vector)
-            output_product(0)
             cell_sum(0)
             gates(1)
             cell_tanh(0)
             brackets(0)
             transposes(0)
             products(1, nc.vector)
-            output_product(1)
             cell_sum(1)
             gates(2)
             multiplied = 0
@@ -254,8 +249,8 @@ def tile_mylstm_v_kernel(
                     load(n + LOAD_AHEAD)
                 if n < GATES:
                     transpose_weights(n)
-                if n + 3 < N_TILES:
-                    gates(n + 3)
+                if n + GATES_AHEAD < N_TILES:
+                    gates(n + GATES_AHEAD)
                 if n + 1 < N_TILES:
                     cell_tanh(n + 1)
                 if n < GATES:
@@ -273,8 +268,6 @@ def tile_mylstm_v_kernel(
                 if n + 2 < N_TILES:
                     products(n + 2, nc.gpsimd)
                 gradients(n)
-                if n + 2 < N_TILES:
-                    output_product(n + 2)
                 if 1 <= n <= GATES:
                     quantise_weights(n - 1)
                 if n + 1 < N_TILES:

@@ -21,6 +21,8 @@ LOAD_AHEAD = 4
 GATES_AHEAD = 3
 FIRST_MX_ROUND = GATES + 1
 MX_TILES_A_ROUND = 2
+RING = 6
+SLOTS = 3
 
 FLOPS = 2 * TOKENS * D * GATES * U
 BYTES = 4 * TOKENS * GATES * U + 2 * 2 * TOKENS * U + 2 * GATES * D * U + 4 * TOKENS * D
@@ -36,7 +38,7 @@ def tile_mylstm_v_kernel(
         const = pools.enter_context(tc.tile_pool(name="const", bufs=1))
         w_pool = pools.enter_context(tc.tile_pool(name="w_pool", bufs=GATES))
         loads = pools.enter_context(tc.tile_pool(name="loads", bufs=LOAD_AHEAD + 1))
-        by_token = pools.enter_context(tc.tile_pool(name="by_token", bufs=2))
+        by_token = pools.enter_context(tc.tile_pool(name="by_token", bufs=3))
         by_unit = pools.enter_context(tc.tile_pool(name="by_unit", bufs=2))
         quantised = pools.enter_context(tc.tile_pool(name="quantised", bufs=FIRST_MX_ROUND + 2))
         results = pools.enter_context(tc.tile_pool(name="results", bufs=MX_TILES_A_ROUND + 1))
@@ -50,9 +52,10 @@ def tile_mylstm_v_kernel(
         w_codes = const.tile([P, GATES, D], U32, align_bytes=64)
         w_scales = const.tile([P, GATES, D], U8, align_bytes=64)
 
-        z_of, cg_of, sig_of, c_tilde_of, c_tilde_sq_of, prod_a_of, prod_bog_of = {}, {}, {}, {}, {}, {}, {}
-        c_new_of, th_of, th_sq_of, brackets_of, banks_of, dz_of, mx_of, acc_of = {}, {}, {}, {}, {}, {}, {}, {}
+        z_of, cg_of, sig_of, c_tilde_of, minus_c_tilde_of, prod_a_of, prod_bog_of, prod_m_of = {}, {}, {}, {}, {}, {}, {}, {}
+        c_new_of, th_of, th_sq_of, bank_of, by_unit_of, dz_of, mx_of, acc_of = {}, {}, {}, {}, {}, {}, {}, {}
         w_rows_of, wt_of, w_grouped_of = {}, {}, {}
+        ring_log = []
 
         def load(n):
             rows = slice(n * P, (n + 1) * P)
@@ -69,27 +72,25 @@ def tile_mylstm_v_kernel(
                 w_rows = w_pool.tile([P, D // P, U], BF16)
                 nc.sync.dma_start(out=w_rows[:], in_=weights[gate].rearrange("(j p) u -> p j u", p=P))
                 w_rows_of[gate] = w_rows
+                w_grouped = w_pool.tile([P, D, PACK], BF16, align_bytes=64)
+                w_grouped_of[gate] = w_grouped
 
-        def transpose_weights(gate):
-            for half in range(2):
-                wt = psum.tile([P, PACK, 2 * P], BF16, tag="acc", bufs=2)
-                for j in range(2):
-                    for t in range(PACK):
-                        nc.tensor.transpose(
-                            wt[:, t, j * P : (j + 1) * P],
-                            w_rows_of[gate][:, 2 * half + j, t * P : (t + 1) * P],
-                            ident_bf16[:],
-                        )
-                wt_of[(gate, half)] = wt
+        def transpose_weights(gate, half):
+            wt = psum.tile([P, PACK, 2 * P], BF16, tag="acc")
+            for j in range(2):
+                for t in range(PACK):
+                    nc.tensor.transpose(
+                        wt[:, t, j * P : (j + 1) * P],
+                        w_rows_of[gate][:, 2 * half + j, t * P : (t + 1) * P],
+                        ident_bf16[:],
+                    )
+            wt_of[(gate, half)] = wt
 
-        def group_weights(gate):
-            w_grouped = w_pool.tile([P, D, PACK], BF16, align_bytes=64)
-            for half in range(2):
-                nc.scalar.copy(
-                    out=w_grouped[:, half * 2 * P : (half + 1) * 2 * P, :],
-                    in_=wt_of[(gate, half)][:].rearrange("p t d -> p d t"),
-                )
-            w_grouped_of[gate] = w_grouped
+        def group_weights(gate, half):
+            nc.scalar.copy(
+                out=w_grouped_of[gate][:, half * 2 * P : (half + 1) * 2 * P, :],
+                in_=wt_of[(gate, half)][:].rearrange("p t d -> p d t"),
+            )
 
         def quantise_weights(gate):
             nc.vector.quantize_mx(
@@ -98,38 +99,66 @@ def tile_mylstm_v_kernel(
                 in_=w_grouped_of[gate][:].rearrange("p d t -> p (d t)"),
             )
 
-        def gates(n):
+        def gates_first(n):
             z_sb = z_of[n]
             sig = by_token.tile([P, 3 * U], F32, bufs=GATES_AHEAD + 1)
             nc.scalar.activation(out=sig[:, 0 : 2 * U], in_=z_sb[:, 0 : 2 * U], func=ACT.Sigmoid)
-            c_tilde = by_token.tile([P, U], F32, bufs=GATES_AHEAD + 1)
+            c_tilde = by_token.tile([P, U], F32)
             nc.scalar.activation(out=c_tilde[:], in_=z_sb[:, 2 * U : 3 * U], func=ACT.Tanh)
-            nc.scalar.activation(out=sig[:, 2 * U : 3 * U], in_=z_sb[:, 3 * U : 4 * U], func=ACT.Sigmoid)
-            c_tilde_sq = by_token.tile([P, U], F32, bufs=GATES_AHEAD + 1)
-            nc.scalar.activation(out=c_tilde_sq[:], in_=c_tilde[:], func=ACT.Square)
-            sig_of[n], c_tilde_of[n], c_tilde_sq_of[n] = sig, c_tilde, c_tilde_sq
+            sig_of[n], c_tilde_of[n] = sig, c_tilde
+
+        def gates_second(n):
+            z_sb = z_of[n]
+            nc.scalar.activation(out=sig_of[n][:, 2 * U : 3 * U], in_=z_sb[:, 3 * U : 4 * U], func=ACT.Sigmoid)
+            minus_c_tilde = by_token.tile([P, U], F32)
+            nc.scalar.activation(out=minus_c_tilde[:], in_=z_sb[:, 2 * U : 3 * U], func=ACT.Tanh, scale=-1.0)
+            minus_c_tilde_of[n] = minus_c_tilde
+
+        def slot(n):
+            return "slot%d" % (n % SLOTS)
 
         def products(n, engine):
             sig = sig_of[n]
-            prod_a = by_token.tile([P, U], F32, bufs=1)
+            prod_a = by_token.tile([P, U], F32, tag=slot(n), bufs=1, align_bytes=64)
             engine.tensor_tensor(out=prod_a[:], in0=sig[:, 0:U], in1=c_tilde_of[n][:], op=ALU.mult)
             prod_bog = by_token.tile([P, 2 * U], F32)
             engine.tensor_tensor(out=prod_bog[:], in0=sig[:, U : 3 * U], in1=cg_of[n][:], op=ALU.mult)
-            prod_a_of[n], prod_bog_of[n] = prod_a, prod_bog
+            prod_m = by_token.tile([P, U], F32)
+            engine.tensor_tensor(out=prod_m[:], in0=prod_a[:], in1=minus_c_tilde_of[n][:], op=ALU.mult)
+            prod_a_of[n], prod_bog_of[n], prod_m_of[n] = prod_a, prod_bog, prod_m
+
+        def transpose_sum(bank, sources):
+            for t in range(PACK):
+                units = slice(t * P, (t + 1) * P)
+                if len(sources) == 1:
+                    nc.tensor.transpose(bank[:, t, :], sources[0][:, units], ident_f32[:])
+                else:
+                    for k, source in enumerate(sources):
+                        nc.tensor.matmul(
+                            out=bank[:, t, :], lhsT=source[:, units], rhs=ident_f32[:],
+                            is_transpose=True, start=(k == 0), stop=(k == len(sources) - 1),
+                        )
 
         def cell_sum(n):
             c_new = psum.tile([P, PACK, P], F32)
-            for t in range(PACK):
-                units = slice(t * P, (t + 1) * P)
-                nc.tensor.matmul(
-                    out=c_new[:, t, :], lhsT=prod_a_of[n][:, units], rhs=ident_f32[:],
-                    is_transpose=True, start=True, stop=False,
-                )
-                nc.tensor.matmul(
-                    out=c_new[:, t, :], lhsT=prod_bog_of[n][:, units], rhs=ident_f32[:],
-                    is_transpose=True, start=False, stop=True,
-                )
+            transpose_sum(c_new, [prod_a_of[n][:], prod_bog_of[n][:, 0:U]])
             c_new_of[n] = c_new
+
+        def ring(n, what):
+            sig = sig_of[n]
+            sources = {
+                "og": [prod_bog_of[n][:, U : 2 * U]],
+                "o": [sig[:, 2 * U : 3 * U]],
+                "i": [sig[:, 0:U]],
+                "f": [sig[:, U : 2 * U]],
+                "a": [prod_a_of[n][:]],
+                "bracket_c": [sig[:, 0:U], prod_m_of[n][:]],
+                "b": [prod_bog_of[n][:, 0:U]],
+            }[what]
+            bank = psum.tile([P, PACK, P], F32, tag="ring%d" % (len(ring_log) % RING))
+            ring_log.append((n, what))
+            transpose_sum(bank, sources)
+            bank_of[(n, what)] = bank
 
         def word_order(bank):
             return bank[:].rearrange("p t b -> p b t")
@@ -141,63 +170,36 @@ def tile_mylstm_v_kernel(
             nc.scalar.activation(out=th_sq[:], in_=th[:], func=ACT.Square)
             th_of[n], th_sq_of[n] = th, th_sq
 
-        def brackets(n):
-            sig = sig_of[n]
-            bracket_c = by_token.tile([P, U], F32)
+        def minus_one_times(n, name, what, other):
+            result = by_unit.tile([P, P, PACK], F32, tag=name)
             nc.vector.scalar_tensor_tensor(
-                out=bracket_c[:], in0=c_tilde_sq_of[n][:], scalar=1.0, in1=sig[:, 0:U],
+                out=result[:], in0=word_order(bank_of[(n, what)]), scalar=1.0, in1=other[:],
                 op0=ALU.subtract, op1=ALU.mult,
             )
-            bracket_f = by_token.tile([P, U], F32)
-            nc.vector.scalar_tensor_tensor(
-                out=bracket_f[:], in0=sig[:, U : 2 * U], scalar=1.0, in1=prod_bog_of[n][:, 0:U],
-                op0=ALU.subtract, op1=ALU.mult,
-            )
-            bracket_i = by_token.tile([P, U], F32)
-            nc.vector.scalar_tensor_tensor(
-                out=bracket_i[:], in0=sig[:, 0:U], scalar=1.0, in1=prod_a_of[n][:],
-                op0=ALU.subtract, op1=ALU.mult,
-            )
-            brackets_of[n] = (bracket_i, bracket_f, bracket_c)
+            by_unit_of[(n, name)] = result
 
-        def transpose_512(bank, by_token_cols):
-            for t in range(PACK):
-                nc.tensor.transpose(bank[:, t, :], by_token_cols[:, t * P : (t + 1) * P], ident_f32[:])
-
-        def transposes(n):
-            bracket_i, bracket_f, bracket_c = brackets_of[n]
-            o_t = psum.tile([P, PACK, P], F32)
-            transpose_512(o_t, sig_of[n][:, 2 * U : 3 * U])
-            bracket_i_t = psum.tile([P, PACK, P], F32)
-            transpose_512(bracket_i_t, bracket_i[:])
-            og_t = psum.tile([P, PACK, P], F32)
-            transpose_512(og_t, prod_bog_of[n][:, U : 2 * U])
-            bracket_f_t = psum.tile([P, PACK, P], F32)
-            transpose_512(bracket_f_t, bracket_f[:])
-            bracket_c_t = psum.tile([P, PACK, P], F32)
-            transpose_512(bracket_c_t, bracket_c[:])
-            banks_of[n] = (o_t, bracket_i_t, og_t, bracket_f_t, bracket_c_t)
-
-        def gradients(n):
-            o_t, bracket_i_t, og_t, bracket_f_t, bracket_c_t = banks_of[n]
-            th = th_of[n]
-            minus_dc = by_unit.tile([P, P, PACK], F32)
+        def minus_dc(n):
+            result = by_unit.tile([P, P, PACK], F32, tag="minus_dc")
             nc.vector.scalar_tensor_tensor(
-                out=minus_dc[:], in0=th_sq_of[n][:], scalar=1.0, in1=word_order(og_t),
+                out=result[:], in0=th_sq_of[n][:], scalar=1.0, in1=word_order(bank_of[(n, "og")]),
                 op0=ALU.subtract, op1=ALU.mult,
             )
-            o_th = by_unit.tile([P, P, PACK], F32)
-            nc.vector.scalar_tensor_tensor(
-                out=o_th[:], in0=word_order(o_t), scalar=1.0, in1=th[:], op0=ALU.subtract, op1=ALU.mult
-            )
-            dz = by_unit.tile([P, GATES, P, PACK], BF16, align_bytes=64)
-            nc.vector.tensor_tensor(out=dz[:, 0], in0=word_order(bracket_i_t), in1=minus_dc[:], op=ALU.mult)
-            nc.vector.scalar_tensor_tensor(
-                out=dz[:, 3], in0=word_order(og_t), scalar=-1.0, in1=o_th[:], op0=ALU.mult, op1=ALU.mult
-            )
-            nc.vector.tensor_tensor(out=dz[:, 1], in0=word_order(bracket_f_t), in1=minus_dc[:], op=ALU.mult)
-            nc.vector.tensor_tensor(out=dz[:, 2], in0=word_order(bracket_c_t), in1=minus_dc[:], op=ALU.mult)
+            by_unit_of[(n, "minus_dc")] = result
+
+        def new_dz(n):
+            dz = by_token.tile([P, GATES, P, PACK], BF16, tag=slot(n), bufs=1, align_bytes=64)
             dz_of[n] = dz
+
+        def gradient(n, gate, what, name, sign):
+            if sign > 0:
+                nc.vector.tensor_tensor(
+                    out=dz_of[n][:, gate], in0=word_order(bank_of[(n, what)]), in1=by_unit_of[(n, name)][:], op=ALU.mult
+                )
+            else:
+                nc.vector.scalar_tensor_tensor(
+                    out=dz_of[n][:, gate], in0=word_order(bank_of[(n, what)]), scalar=-1.0,
+                    in1=by_unit_of[(n, name)][:], op0=ALU.mult, op1=ALU.mult,
+                )
 
         def quantise(n):
             dz_codes = quantised.tile([P, GATES, P], U32, align_bytes=64)
@@ -211,7 +213,7 @@ def tile_mylstm_v_kernel(
 
         def multiply(n):
             dz_codes, dz_scales = mx_of[n]
-            acc = psum.tile([P, D], F32, tag="acc", bufs=2)
+            acc = psum.tile([P, D], F32, tag="acc")
             for gate in range(GATES):
                 nc.tensor.matmul_mx(
                     out=acc[:],
@@ -233,45 +235,73 @@ def tile_mylstm_v_kernel(
             for n in range(LOAD_AHEAD):
                 load(n)
             load_weights()
-            gates(0)
+            gates_first(0)
+            gates_second(0)
             products(0, nc.vector)
             cell_sum(0)
-            gates(1)
+            gates_first(1)
+            gates_second(1)
             cell_tanh(0)
-            brackets(0)
-            transposes(0)
+            for what in ("og", "o", "i", "f", "a"):
+                ring(0, what)
             products(1, nc.vector)
             cell_sum(1)
-            gates(2)
+            gates_first(2)
+            gates_second(2)
             multiplied = 0
             for n in range(N_TILES):
+                more = n + 1 < N_TILES
                 if n + LOAD_AHEAD < N_TILES:
                     load(n + LOAD_AHEAD)
-                if n < GATES:
-                    transpose_weights(n)
-                if n + GATES_AHEAD < N_TILES:
-                    gates(n + GATES_AHEAD)
-                if n + 1 < N_TILES:
+                if more:
                     cell_tanh(n + 1)
+                ring(n, "bracket_c")
                 if n < GATES:
-                    group_weights(n)
-                if n + 1 < N_TILES:
-                    brackets(n + 1)
+                    transpose_weights(n, 0)
+                    group_weights(n, 0)
+                minus_dc(n)
+                minus_one_times(n, "o_th", "o", th_of[n])
+                if 1 <= n <= GATES:
+                    quantise_weights(n - 1)
                 if n >= 1:
                     quantise(n - 1)
                 first_of_round = multiplied
                 if n >= FIRST_MX_ROUND:
                     multiplied = min(n, first_of_round + MX_TILES_A_ROUND)
-                for m in range(first_of_round, multiplied):
-                    multiply(m)
-                    store(m)
+                if multiplied > first_of_round:
+                    multiply(first_of_round)
                 if n + 2 < N_TILES:
                     products(n + 2, nc.gpsimd)
-                gradients(n)
-                if 1 <= n <= GATES:
-                    quantise_weights(n - 1)
-                if n + 1 < N_TILES:
-                    transposes(n + 1)
+                if n + GATES_AHEAD < N_TILES:
+                    gates_first(n + GATES_AHEAD)
+                minus_one_times(n, "e_i", "i", by_unit_of[(n, "minus_dc")])
+                new_dz(n)
+                gradient(n, 3, "og", "o_th", -1)
+                ring(n, "b")
+                if more:
+                    ring(n + 1, "og")
+                    ring(n + 1, "o")
+                if multiplied > first_of_round:
+                    store(first_of_round)
+                if n < GATES:
+                    transpose_weights(n, 1)
+                    group_weights(n, 1)
+                if multiplied > first_of_round + 1:
+                    multiply(first_of_round + 1)
+                minus_one_times(n, "e_f", "f", by_unit_of[(n, "minus_dc")])
+                if more:
+                    ring(n + 1, "i")
+                gradient(n, 0, "a", "e_i", 1)
+                if more:
+                    ring(n + 1, "f")
+                gradient(n, 2, "bracket_c", "minus_dc", -1)
+                if more:
+                    ring(n + 1, "a")
+                gradient(n, 1, "b", "e_f", 1)
+                if n + GATES_AHEAD < N_TILES:
+                    gates_second(n + GATES_AHEAD)
+                if multiplied > first_of_round + 1:
+                    store(first_of_round + 1)
                 if n + 2 < N_TILES:
                     cell_sum(n + 2)
             quantise(N_TILES - 1)

@@ -52,7 +52,7 @@ def tile_mylstm_v_kernel(
         w_codes = const.tile([P, GATES, D], U32, align_bytes=64)
         w_scales = const.tile([P, GATES, D], U8, align_bytes=64)
 
-        z_of, cg_of, sig_of, c_tilde_of, minus_c_tilde_of, prod_a_of, prod_bog_of, prod_m_of = {}, {}, {}, {}, {}, {}, {}, {}
+        z_of, cg_of, sig_of, c_tilde_of, c_tilde_sq_of, prod_a_of, prod_bog_of, brackets_of = {}, {}, {}, {}, {}, {}, {}, {}
         c_new_of, th_of, th_sq_of, bank_of, by_unit_of, dz_of, mx_of, acc_of = {}, {}, {}, {}, {}, {}, {}, {}
         w_rows_of, wt_of, w_grouped_of = {}, {}, {}
         ring_log = []
@@ -110,9 +110,9 @@ def tile_mylstm_v_kernel(
         def gates_second(n):
             z_sb = z_of[n]
             nc.scalar.activation(out=sig_of[n][:, 2 * U : 3 * U], in_=z_sb[:, 3 * U : 4 * U], func=ACT.Sigmoid)
-            minus_c_tilde = by_token.tile([P, U], F32)
-            nc.scalar.activation(out=minus_c_tilde[:], in_=z_sb[:, 2 * U : 3 * U], func=ACT.Tanh, scale=-1.0)
-            minus_c_tilde_of[n] = minus_c_tilde
+            c_tilde_sq = by_token.tile([P, U], F32)
+            nc.scalar.activation(out=c_tilde_sq[:], in_=c_tilde_of[n][:], func=ACT.Square)
+            c_tilde_sq_of[n] = c_tilde_sq
 
         def slot(n):
             return "slot%d" % (n % SLOTS)
@@ -123,9 +123,21 @@ def tile_mylstm_v_kernel(
             engine.tensor_tensor(out=prod_a[:], in0=sig[:, 0:U], in1=c_tilde_of[n][:], op=ALU.mult)
             prod_bog = by_token.tile([P, 2 * U], F32)
             engine.tensor_tensor(out=prod_bog[:], in0=sig[:, U : 3 * U], in1=cg_of[n][:], op=ALU.mult)
-            prod_m = by_token.tile([P, U], F32)
-            engine.tensor_tensor(out=prod_m[:], in0=prod_a[:], in1=minus_c_tilde_of[n][:], op=ALU.mult)
-            prod_a_of[n], prod_bog_of[n], prod_m_of[n] = prod_a, prod_bog, prod_m
+            prod_a_of[n], prod_bog_of[n] = prod_a, prod_bog
+
+        def brackets(n):
+            sig = sig_of[n]
+            bracket_c = by_token.tile([P, U], F32, bufs=2)
+            nc.vector.scalar_tensor_tensor(
+                out=bracket_c[:], in0=c_tilde_sq_of[n][:], scalar=1.0, in1=sig[:, 0:U],
+                op0=ALU.subtract, op1=ALU.mult,
+            )
+            bracket_f = by_token.tile([P, U], F32, bufs=2)
+            nc.vector.scalar_tensor_tensor(
+                out=bracket_f[:], in0=sig[:, U : 2 * U], scalar=1.0, in1=prod_bog_of[n][:, 0:U],
+                op0=ALU.subtract, op1=ALU.mult,
+            )
+            brackets_of[n] = (bracket_f, bracket_c)
 
         def transpose_sum(bank, sources):
             for t in range(PACK):
@@ -150,10 +162,9 @@ def tile_mylstm_v_kernel(
                 "og": [prod_bog_of[n][:, U : 2 * U]],
                 "o": [sig[:, 2 * U : 3 * U]],
                 "i": [sig[:, 0:U]],
-                "f": [sig[:, U : 2 * U]],
                 "a": [prod_a_of[n][:]],
-                "bracket_c": [sig[:, 0:U], prod_m_of[n][:]],
-                "b": [prod_bog_of[n][:, 0:U]],
+                "bracket_f": [brackets_of[n][0][:]],
+                "bracket_c": [brackets_of[n][1][:]],
             }[what]
             bank = psum.tile([P, PACK, P], F32, tag="ring%d" % (len(ring_log) % RING))
             ring_log.append((n, what))
@@ -242,7 +253,8 @@ def tile_mylstm_v_kernel(
             gates_first(1)
             gates_second(1)
             cell_tanh(0)
-            for what in ("og", "o", "i", "f", "a"):
+            brackets(0)
+            for what in ("o", "i", "og", "a", "bracket_f", "bracket_c"):
                 ring(0, what)
             products(1, nc.vector)
             cell_sum(1)
@@ -255,53 +267,54 @@ def tile_mylstm_v_kernel(
                     load(n + LOAD_AHEAD)
                 if more:
                     cell_tanh(n + 1)
-                ring(n, "bracket_c")
                 if n < GATES:
                     transpose_weights(n, 0)
                     group_weights(n, 0)
-                minus_dc(n)
-                minus_one_times(n, "o_th", "o", th_of[n])
-                if 1 <= n <= GATES:
-                    quantise_weights(n - 1)
-                if n >= 1:
-                    quantise(n - 1)
                 first_of_round = multiplied
                 if n >= FIRST_MX_ROUND:
                     multiplied = min(n, first_of_round + MX_TILES_A_ROUND)
-                if multiplied > first_of_round:
+                if multiplied > first_of_round + 1:
                     multiply(first_of_round)
+                    store(first_of_round)
+                if more:
+                    brackets(n + 1)
+                if n >= 1:
+                    quantise(n - 1)
                 if n + 2 < N_TILES:
                     products(n + 2, nc.gpsimd)
                 if n + GATES_AHEAD < N_TILES:
                     gates_first(n + GATES_AHEAD)
+                minus_dc(n)
+                minus_one_times(n, "o_th", "o", th_of[n])
+                if more:
+                    ring(n + 1, "o")
                 minus_one_times(n, "e_i", "i", by_unit_of[(n, "minus_dc")])
+                if more:
+                    ring(n + 1, "i")
                 new_dz(n)
                 gradient(n, 3, "og", "o_th", -1)
-                ring(n, "b")
                 if more:
                     ring(n + 1, "og")
-                    ring(n + 1, "o")
                 if multiplied > first_of_round:
-                    store(first_of_round)
+                    multiply(multiplied - 1)
                 if n < GATES:
                     transpose_weights(n, 1)
                     group_weights(n, 1)
-                if multiplied > first_of_round + 1:
-                    multiply(first_of_round + 1)
-                minus_one_times(n, "e_f", "f", by_unit_of[(n, "minus_dc")])
-                if more:
-                    ring(n + 1, "i")
                 gradient(n, 0, "a", "e_i", 1)
                 if more:
-                    ring(n + 1, "f")
-                gradient(n, 2, "bracket_c", "minus_dc", -1)
-                if more:
                     ring(n + 1, "a")
-                gradient(n, 1, "b", "e_f", 1)
+                gradient(n, 1, "bracket_f", "minus_dc", 1)
+                if more:
+                    ring(n + 1, "bracket_f")
+                gradient(n, 2, "bracket_c", "minus_dc", 1)
+                if more:
+                    ring(n + 1, "bracket_c")
+                if 1 <= n <= GATES:
+                    quantise_weights(n - 1)
                 if n + GATES_AHEAD < N_TILES:
                     gates_second(n + GATES_AHEAD)
-                if multiplied > first_of_round + 1:
-                    store(first_of_round + 1)
+                if multiplied > first_of_round:
+                    store(multiplied - 1)
                 if n + 2 < N_TILES:
                     cell_sum(n + 2)
             quantise(N_TILES - 1)

@@ -212,30 +212,48 @@ def tile_mylstm_v_kernel(
                     in1=by_unit_of[(n, name)][:], op0=ALU.mult, op1=ALU.mult,
                 )
 
-        def quantise(n):
+        def new_codes(n):
             dz_codes = quantised.tile([P, GATES, P], U32, align_bytes=64)
             dz_scales = quantised.tile([P, GATES, P], U8, align_bytes=64)
+            mx_of[n] = (dz_codes, dz_scales)
+
+        def quantise(n):
+            new_codes(n)
+            dz_codes, dz_scales = mx_of[n]
             nc.vector.quantize_mx(
                 out=dz_codes[:].rearrange("p g b -> p (g b)").bitcast(E5M2_X4),
                 scales=dz_scales[:].rearrange("p g b -> p (g b)"),
                 in_=dz_of[n][:].rearrange("p g b t -> p (g b t)"),
             )
-            mx_of[n] = (dz_codes, dz_scales)
+
+        def quantise_gate(n, gate):
+            dz_codes, dz_scales = mx_of[n]
+            nc.vector.quantize_mx(
+                out=dz_codes[:, gate, :].bitcast(E5M2_X4),
+                scales=dz_scales[:, gate, :],
+                in_=dz_of[n][:, gate].rearrange("p b t -> p (b t)"),
+            )
+
+        def new_acc(n):
+            acc = psum.tile([P, D], F32, tag="acc")
+            acc_of[n] = acc
+
+        def multiply_gate(n, gate, first, last):
+            dz_codes, dz_scales = mx_of[n]
+            nc.tensor.matmul_mx(
+                out=acc_of[n][:],
+                lhsT=dz_codes[:, gate, :].bitcast(E5M2_X4),
+                lhsT_scale=dz_scales[:, gate, :],
+                rhs=w_codes[:, gate, :].bitcast(E4M3_X4),
+                rhs_scale=w_scales[:, gate, :],
+                start=first,
+                stop=last,
+            )
 
         def multiply(n):
-            dz_codes, dz_scales = mx_of[n]
-            acc = psum.tile([P, D], F32, tag="acc")
+            new_acc(n)
             for gate in range(GATES):
-                nc.tensor.matmul_mx(
-                    out=acc[:],
-                    lhsT=dz_codes[:, gate, :].bitcast(E5M2_X4),
-                    lhsT_scale=dz_scales[:, gate, :],
-                    rhs=w_codes[:, gate, :].bitcast(E4M3_X4),
-                    rhs_scale=w_scales[:, gate, :],
-                    start=(gate == 0),
-                    stop=(gate == GATES - 1),
-                )
-            acc_of[n] = acc
+                multiply_gate(n, gate, gate == 0, gate == GATES - 1)
 
         def store(n):
             out_rows = results.tile([P, D], F32)
@@ -303,9 +321,14 @@ def tile_mylstm_v_kernel(
                 gradient(n, 0, "a", "e_i", 1)
                 if more:
                     ring(n + 1, "a")
+                else:
+                    new_codes(n)
+                    quantise_gate(n, 3)
                 gradient(n, 1, "bracket_f", "minus_dc", 1)
                 if more:
                     ring(n + 1, "bracket_f")
+                else:
+                    quantise_gate(n, 0)
                 gradient(n, 2, "bracket_c", "minus_dc", 1)
                 if more:
                     ring(n + 1, "bracket_c")
@@ -317,6 +340,12 @@ def tile_mylstm_v_kernel(
                     store(multiplied - 1)
                 if n + 2 < N_TILES:
                     cell_sum(n + 2)
-            quantise(N_TILES - 1)
-            multiply(N_TILES - 1)
-            store(N_TILES - 1)
+            last_tile = N_TILES - 1
+            new_acc(last_tile)
+            multiply_gate(last_tile, 3, True, False)
+            multiply_gate(last_tile, 0, False, False)
+            quantise_gate(last_tile, 1)
+            multiply_gate(last_tile, 1, False, False)
+            quantise_gate(last_tile, 2)
+            multiply_gate(last_tile, 2, False, True)
+            store(last_tile)

@@ -21,7 +21,9 @@ LOAD_AHEAD = 4
 GATES_AHEAD = 3
 FIRST_MX_ROUND = GATES + 1
 MX_TILES_A_ROUND = 2
-RING = 6
+RING = 5
+SPLIT_FROM = 7
+GPSIMD_UNITS = 256
 SLOTS = 3
 
 FLOPS = 2 * TOKENS * D * GATES * U
@@ -54,7 +56,7 @@ def tile_mylstm_v_kernel(
 
         z_of, cg_of, sig_of, c_tilde_of, c_tilde_sq_of, prod_a_of, prod_bog_of, brackets_of = {}, {}, {}, {}, {}, {}, {}, {}
         c_new_of, th_of, th_sq_of, bank_of, by_unit_of, dz_of, mx_of, acc_of = {}, {}, {}, {}, {}, {}, {}, {}
-        w_rows_of, wt_of, w_grouped_of = {}, {}, {}
+        w_rows_of, wt_of, w_grouped_of, f_minus_one_of = {}, {}, {}, {}
         ring_log = []
 
         def load(n):
@@ -76,7 +78,7 @@ def tile_mylstm_v_kernel(
                 w_grouped_of[gate] = w_grouped
 
         def transpose_weights(gate, half):
-            wt = psum.tile([P, PACK, 2 * P], BF16, tag="acc")
+            wt = psum.tile([P, PACK, 2 * P], BF16, tag="acc", bufs=2)
             for j in range(2):
                 for t in range(PACK):
                     nc.tensor.transpose(
@@ -113,6 +115,10 @@ def tile_mylstm_v_kernel(
             c_tilde_sq = by_token.tile([P, U], F32)
             nc.scalar.activation(out=c_tilde_sq[:], in_=c_tilde_of[n][:], func=ACT.Square)
             c_tilde_sq_of[n] = c_tilde_sq
+            if n >= SPLIT_FROM:
+                f_minus_one = by_token.tile([P, GPSIMD_UNITS], F32)
+                nc.scalar.add(out=f_minus_one[:], in_=sig_of[n][:, 2 * U - GPSIMD_UNITS : 2 * U], add=-1.0)
+                f_minus_one_of[n] = f_minus_one
 
         def slot(n):
             return "slot%d" % (n % SLOTS)
@@ -124,20 +130,20 @@ def tile_mylstm_v_kernel(
             prod_bog = by_token.tile([P, 2 * U], F32)
             engine.tensor_tensor(out=prod_bog[:], in0=sig[:, U : 3 * U], in1=cg_of[n][:], op=ALU.mult)
             prod_a_of[n], prod_bog_of[n] = prod_a, prod_bog
+            bracket_f = by_token.tile([P, U], F32)
+            brackets_of[n] = bracket_f
+            if n >= SPLIT_FROM:
+                theirs = slice(U - GPSIMD_UNITS, U)
+                engine.tensor_tensor(
+                    out=bracket_f[:, theirs], in0=f_minus_one_of[n][:], in1=prod_bog[:, theirs], op=ALU.mult
+                )
 
         def brackets(n):
-            sig = sig_of[n]
-            bracket_c = by_token.tile([P, U], F32, bufs=2)
+            ours = U - GPSIMD_UNITS if n >= SPLIT_FROM else U
             nc.vector.scalar_tensor_tensor(
-                out=bracket_c[:], in0=c_tilde_sq_of[n][:], scalar=1.0, in1=sig[:, 0:U],
-                op0=ALU.subtract, op1=ALU.mult,
+                out=brackets_of[n][:, 0:ours], in0=sig_of[n][:, U : U + ours], scalar=1.0,
+                in1=prod_bog_of[n][:, 0:ours], op0=ALU.subtract, op1=ALU.mult,
             )
-            bracket_f = by_token.tile([P, U], F32, bufs=2)
-            nc.vector.scalar_tensor_tensor(
-                out=bracket_f[:], in0=sig[:, U : 2 * U], scalar=1.0, in1=prod_bog_of[n][:, 0:U],
-                op0=ALU.subtract, op1=ALU.mult,
-            )
-            brackets_of[n] = (bracket_f, bracket_c)
 
         def transpose_sum(bank, sources):
             for t in range(PACK):
@@ -162,9 +168,9 @@ def tile_mylstm_v_kernel(
                 "og": [prod_bog_of[n][:, U : 2 * U]],
                 "o": [sig[:, 2 * U : 3 * U]],
                 "i": [sig[:, 0:U]],
-                "a": [prod_a_of[n][:]],
-                "bracket_f": [brackets_of[n][0][:]],
-                "bracket_c": [brackets_of[n][1][:]],
+                "c_tilde_sq": [c_tilde_sq_of[n][:]],
+                "c_tilde": [c_tilde_of[n][:]],
+                "bracket_f": [brackets_of[n][:]],
             }[what]
             bank = psum.tile([P, PACK, P], F32, tag="ring%d" % (len(ring_log) % RING))
             ring_log.append((n, what))
@@ -189,6 +195,11 @@ def tile_mylstm_v_kernel(
             )
             by_unit_of[(n, name)] = result
 
+        def times(n, name, what, other):
+            result = by_unit.tile([P, P, PACK], F32, tag=name)
+            nc.vector.tensor_tensor(out=result[:], in0=word_order(bank_of[(n, what)]), in1=other[:], op=ALU.mult)
+            by_unit_of[(n, name)] = result
+
         def minus_dc(n):
             result = by_unit.tile([P, P, PACK], F32, tag="minus_dc")
             nc.vector.scalar_tensor_tensor(
@@ -200,6 +211,12 @@ def tile_mylstm_v_kernel(
         def new_dz(n):
             dz = by_token.tile([P, GATES, P, PACK], BF16, tag=slot(n), bufs=1, align_bytes=64)
             dz_of[n] = dz
+
+        def gradient_minus_one(n, gate, what, name):
+            nc.vector.scalar_tensor_tensor(
+                out=dz_of[n][:, gate], in0=word_order(bank_of[(n, what)]), scalar=1.0,
+                in1=by_unit_of[(n, name)][:], op0=ALU.subtract, op1=ALU.mult,
+            )
 
         def gradient(n, gate, what, name, sign):
             if sign > 0:
@@ -235,7 +252,7 @@ def tile_mylstm_v_kernel(
             )
 
         def new_acc(n):
-            acc = psum.tile([P, D], F32, tag="acc")
+            acc = psum.tile([P, D], F32, tag="acc", bufs=2)
             acc_of[n] = acc
 
         def multiply_gate(n, gate, first, last):
@@ -272,7 +289,7 @@ def tile_mylstm_v_kernel(
             gates_second(1)
             cell_tanh(0)
             brackets(0)
-            for what in ("o", "i", "og", "a", "bracket_f", "bracket_c"):
+            for what in ("og", "o", "i", "c_tilde_sq"):
                 ring(0, what)
             products(1, nc.vector)
             cell_sum(1)
@@ -285,67 +302,65 @@ def tile_mylstm_v_kernel(
                     load(n + LOAD_AHEAD)
                 if more:
                     cell_tanh(n + 1)
-                if n < GATES:
-                    transpose_weights(n, 0)
-                    group_weights(n, 0)
+                ring(n, "c_tilde")
                 first_of_round = multiplied
                 if n >= FIRST_MX_ROUND:
                     multiplied = min(n, first_of_round + MX_TILES_A_ROUND)
                 if multiplied > first_of_round + 1:
                     multiply(first_of_round)
                     store(first_of_round)
-                if more:
-                    brackets(n + 1)
+                minus_dc(n)
                 if n >= 1:
                     quantise(n - 1)
+                if more:
+                    brackets(n + 1)
+                if multiplied > first_of_round:
+                    multiply(multiplied - 1)
                 if n + 2 < N_TILES:
                     products(n + 2, nc.gpsimd)
                 if n + GATES_AHEAD < N_TILES:
                     gates_first(n + GATES_AHEAD)
-                minus_dc(n)
                 minus_one_times(n, "o_th", "o", th_of[n])
-                if more:
-                    ring(n + 1, "o")
-                minus_one_times(n, "e_i", "i", by_unit_of[(n, "minus_dc")])
-                if more:
-                    ring(n + 1, "i")
+                times(n, "y", "i", by_unit_of[(n, "minus_dc")])
                 new_dz(n)
                 gradient(n, 3, "og", "o_th", -1)
+                ring(n, "bracket_f")
                 if more:
                     ring(n + 1, "og")
                 if multiplied > first_of_round:
-                    multiply(multiplied - 1)
-                if n < GATES:
-                    transpose_weights(n, 1)
-                    group_weights(n, 1)
-                gradient(n, 0, "a", "e_i", 1)
+                    store(multiplied - 1)
+                minus_one_times(n, "w", "i", by_unit_of[(n, "y")])
                 if more:
-                    ring(n + 1, "a")
+                    ring(n + 1, "o")
+                gradient_minus_one(n, 2, "c_tilde_sq", "y")
+                if more:
+                    ring(n + 1, "i")
                 else:
                     new_codes(n)
                     quantise_gate(n, 3)
-                gradient(n, 1, "bracket_f", "minus_dc", 1)
+                gradient(n, 0, "c_tilde", "w", 1)
                 if more:
-                    ring(n + 1, "bracket_f")
+                    ring(n + 1, "c_tilde_sq")
                 else:
-                    quantise_gate(n, 0)
-                gradient(n, 2, "bracket_c", "minus_dc", 1)
-                if more:
-                    ring(n + 1, "bracket_c")
+                    quantise_gate(n, 2)
+                gradient(n, 1, "bracket_f", "minus_dc", 1)
                 if 1 <= n <= GATES:
                     quantise_weights(n - 1)
                 if n + GATES_AHEAD < N_TILES:
                     gates_second(n + GATES_AHEAD)
-                if multiplied > first_of_round:
-                    store(multiplied - 1)
                 if n + 2 < N_TILES:
                     cell_sum(n + 2)
+                if n < GATES:
+                    transpose_weights(n, 0)
+                    transpose_weights(n, 1)
+                    group_weights(n, 0)
+                    group_weights(n, 1)
             last_tile = N_TILES - 1
             new_acc(last_tile)
             multiply_gate(last_tile, 3, True, False)
+            multiply_gate(last_tile, 2, False, False)
+            quantise_gate(last_tile, 0)
             multiply_gate(last_tile, 0, False, False)
             quantise_gate(last_tile, 1)
-            multiply_gate(last_tile, 1, False, False)
-            quantise_gate(last_tile, 2)
-            multiply_gate(last_tile, 2, False, True)
+            multiply_gate(last_tile, 1, False, True)
             store(last_tile)

@@ -24,6 +24,7 @@ MX_TILES_A_ROUND = 2
 RING = 5
 SPLIT_FROM = 7
 GPSIMD_UNITS = 256
+FINE_TILES = 2
 SLOTS = 3
 
 FLOPS = 2 * TOKENS * D * GATES * U
@@ -63,9 +64,16 @@ def tile_mylstm_v_kernel(
             rows = slice(n * P, (n + 1) * P)
             z_sb = loads.tile([P, GATES * U], F32)
             cg = loads.tile([P, 2 * U], BF16)
-            nc.sync.dma_start(out=z_sb[:, 0 : 2 * U], in_=z[rows, 0 : 2 * U])
-            nc.sync.dma_start(out=cg[:, 0:U], in_=c[rows, :])
-            nc.sync.dma_start(out=z_sb[:, 2 * U : 4 * U], in_=z[rows, 2 * U : 4 * U])
+            if n < FINE_TILES:
+                nc.sync.dma_start(out=z_sb[:, 0:U], in_=z[rows, 0:U])
+                nc.sync.dma_start(out=z_sb[:, 2 * U : 3 * U], in_=z[rows, 2 * U : 3 * U])
+                nc.sync.dma_start(out=z_sb[:, U : 2 * U], in_=z[rows, U : 2 * U])
+                nc.sync.dma_start(out=cg[:, 0:U], in_=c[rows, :])
+                nc.sync.dma_start(out=z_sb[:, 3 * U : 4 * U], in_=z[rows, 3 * U : 4 * U])
+            else:
+                nc.sync.dma_start(out=z_sb[:, 0 : 2 * U], in_=z[rows, 0 : 2 * U])
+                nc.sync.dma_start(out=cg[:, 0:U], in_=c[rows, :])
+                nc.sync.dma_start(out=z_sb[:, 2 * U : 4 * U], in_=z[rows, 2 * U : 4 * U])
             nc.sync.dma_start(out=cg[:, U : 2 * U], in_=grad_out[rows, :])
             z_of[n], cg_of[n] = z_sb, cg
 
@@ -104,17 +112,27 @@ def tile_mylstm_v_kernel(
         def gates_first(n):
             z_sb = z_of[n]
             sig = by_token.tile([P, 3 * U], F32, bufs=GATES_AHEAD + 1)
-            nc.scalar.activation(out=sig[:, 0 : 2 * U], in_=z_sb[:, 0 : 2 * U], func=ACT.Sigmoid)
             c_tilde = by_token.tile([P, U], F32)
-            nc.scalar.activation(out=c_tilde[:], in_=z_sb[:, 2 * U : 3 * U], func=ACT.Tanh)
+            if n < FINE_TILES:
+                nc.scalar.activation(out=sig[:, 0:U], in_=z_sb[:, 0:U], func=ACT.Sigmoid)
+                nc.scalar.activation(out=c_tilde[:], in_=z_sb[:, 2 * U : 3 * U], func=ACT.Tanh)
+                nc.scalar.activation(out=sig[:, U : 2 * U], in_=z_sb[:, U : 2 * U], func=ACT.Sigmoid)
+            else:
+                nc.scalar.activation(out=sig[:, 0 : 2 * U], in_=z_sb[:, 0 : 2 * U], func=ACT.Sigmoid)
+                nc.scalar.activation(out=c_tilde[:], in_=z_sb[:, 2 * U : 3 * U], func=ACT.Tanh)
             sig_of[n], c_tilde_of[n] = sig, c_tilde
 
-        def gates_second(n):
-            z_sb = z_of[n]
-            nc.scalar.activation(out=sig_of[n][:, 2 * U : 3 * U], in_=z_sb[:, 3 * U : 4 * U], func=ACT.Sigmoid)
+        def gate_o(n):
+            nc.scalar.activation(out=sig_of[n][:, 2 * U : 3 * U], in_=z_of[n][:, 3 * U : 4 * U], func=ACT.Sigmoid)
+
+        def gate_square(n):
             c_tilde_sq = by_token.tile([P, U], F32)
             nc.scalar.activation(out=c_tilde_sq[:], in_=c_tilde_of[n][:], func=ACT.Square)
             c_tilde_sq_of[n] = c_tilde_sq
+
+        def gates_second(n):
+            gate_o(n)
+            gate_square(n)
             if n >= SPLIT_FROM:
                 f_minus_one = by_token.tile([P, GPSIMD_UNITS], F32)
                 nc.scalar.add(out=f_minus_one[:], in_=sig_of[n][:, 2 * U - GPSIMD_UNITS : 2 * U], add=-1.0)
@@ -128,7 +146,10 @@ def tile_mylstm_v_kernel(
             prod_a = by_token.tile([P, U], F32, tag=slot(n), bufs=1, align_bytes=64)
             engine.tensor_tensor(out=prod_a[:], in0=sig[:, 0:U], in1=c_tilde_of[n][:], op=ALU.mult)
             prod_bog = by_token.tile([P, 2 * U], F32)
-            engine.tensor_tensor(out=prod_bog[:], in0=sig[:, U : 3 * U], in1=cg_of[n][:], op=ALU.mult)
+            if n < FINE_TILES:
+                engine.tensor_tensor(out=prod_bog[:, 0:U], in0=sig[:, U : 2 * U], in1=cg_of[n][:, 0:U], op=ALU.mult)
+            else:
+                engine.tensor_tensor(out=prod_bog[:], in0=sig[:, U : 3 * U], in1=cg_of[n][:], op=ALU.mult)
             prod_a_of[n], prod_bog_of[n] = prod_a, prod_bog
             bracket_f = by_token.tile([P, U], F32)
             brackets_of[n] = bracket_f
@@ -137,6 +158,11 @@ def tile_mylstm_v_kernel(
                 engine.tensor_tensor(
                     out=bracket_f[:, theirs], in0=f_minus_one_of[n][:], in1=prod_bog[:, theirs], op=ALU.mult
                 )
+
+        def product_og(n):
+            nc.vector.tensor_tensor(
+                out=prod_bog_of[n][:, U : 2 * U], in0=sig_of[n][:, 2 * U : 3 * U], in1=cg_of[n][:, U : 2 * U], op=ALU.mult
+            )
 
         def brackets(n):
             ours = U - GPSIMD_UNITS if n >= SPLIT_FROM else U
@@ -165,13 +191,13 @@ def tile_mylstm_v_kernel(
         def ring(n, what):
             sig = sig_of[n]
             sources = {
-                "og": [prod_bog_of[n][:, U : 2 * U]],
-                "o": [sig[:, 2 * U : 3 * U]],
-                "i": [sig[:, 0:U]],
-                "c_tilde_sq": [c_tilde_sq_of[n][:]],
-                "c_tilde": [c_tilde_of[n][:]],
-                "bracket_f": [brackets_of[n][:]],
-            }[what]
+                "og": lambda: [prod_bog_of[n][:, U : 2 * U]],
+                "o": lambda: [sig[:, 2 * U : 3 * U]],
+                "i": lambda: [sig[:, 0:U]],
+                "c_tilde_sq": lambda: [c_tilde_sq_of[n][:]],
+                "c_tilde": lambda: [c_tilde_of[n][:]],
+                "bracket_f": lambda: [brackets_of[n][:]],
+            }[what]()
             bank = psum.tile([P, PACK, P], F32, tag="ring%d" % (len(ring_log) % RING))
             ring_log.append((n, what))
             transpose_sum(bank, sources)
@@ -282,19 +308,24 @@ def tile_mylstm_v_kernel(
                 load(n)
             load_weights()
             gates_first(0)
-            gates_second(0)
+            gate_o(0)
             products(0, nc.vector)
             cell_sum(0)
+            product_og(0)
             gates_first(1)
-            gates_second(1)
-            cell_tanh(0)
             brackets(0)
-            for what in ("og", "o", "i", "c_tilde_sq"):
+            cell_tanh(0)
+            for what in ("og", "o", "i"):
                 ring(0, what)
             products(1, nc.vector)
             cell_sum(1)
+            brackets(1)
+            gate_o(1)
+            gate_square(0)
+            ring(0, "c_tilde_sq")
             gates_first(2)
             gates_second(2)
+            gate_square(1)
             multiplied = 0
             for n in range(N_TILES):
                 more = n + 1 < N_TILES
@@ -312,7 +343,9 @@ def tile_mylstm_v_kernel(
                 minus_dc(n)
                 if n >= 1:
                     quantise(n - 1)
-                if more:
+                if n == 0:
+                    product_og(1)
+                elif more:
                     brackets(n + 1)
                 if multiplied > first_of_round:
                     multiply(multiplied - 1)

@@ -301,7 +301,7 @@ def tile_mylstm_v_kernel(
         def store(n):
             out_rows = results.tile([P, D], F32)
             nc.scalar.copy(out=out_rows[:], in_=acc_of[n][:])
-            nc.scalar.dma_start(out=out[n * P : (n + 1) * P, :], in_=out_rows[:])
+            nc.sync.dma_start(out=out[n * P : (n + 1) * P, :], in_=out_rows[:])
 
         with tc.manual_schedule():
             for n in range(LOAD_AHEAD):

@@ -25,6 +25,15 @@ RING = 5
 SPLIT_FROM = 7
 GPSIMD_UNITS = 256
 FINE_TILES = 2
+INHERITS = {
+    "bracket_f": (0, "o"),
+    "og": (1, "og"),
+    "o": (1, "i"),
+    "i": (1, "c_tilde_sq"),
+    "c_tilde_sq": (1, "c_tilde"),
+    "c_tilde": (1, "bracket_f"),
+}
+FIRST_BANKS = {(0, "og"): 0, (0, "o"): 1, (0, "i"): 2, (0, "c_tilde_sq"): 3, (0, "c_tilde"): 4}
 SLOTS = 3
 
 FLOPS = 2 * TOKENS * D * GATES * U
@@ -58,7 +67,7 @@ def tile_mylstm_v_kernel(
         z_of, cg_of, sig_of, c_tilde_of, c_tilde_sq_of, prod_a_of, prod_bog_of, brackets_of = {}, {}, {}, {}, {}, {}, {}, {}
         c_new_of, th_of, th_sq_of, bank_of, by_unit_of, dz_of, mx_of, acc_of = {}, {}, {}, {}, {}, {}, {}, {}
         w_rows_of, wt_of, w_grouped_of, f_minus_one_of = {}, {}, {}, {}
-        ring_log = []
+        bank_number = {}
 
         def load(n):
             rows = slice(n * P, (n + 1) * P)
@@ -198,8 +207,12 @@ def tile_mylstm_v_kernel(
                 "c_tilde": lambda: [c_tilde_of[n][:]],
                 "bracket_f": lambda: [brackets_of[n][:]],
             }[what]()
-            bank = psum.tile([P, PACK, P], F32, tag="ring%d" % (len(ring_log) % RING))
-            ring_log.append((n, what))
+            if (n, what) in FIRST_BANKS:
+                bank_number[(n, what)] = FIRST_BANKS[(n, what)]
+            else:
+                tiles_back, heir_of = INHERITS[what]
+                bank_number[(n, what)] = bank_number[(n - tiles_back, heir_of)]
+            bank = psum.tile([P, PACK, P], F32, tag="ring%d" % bank_number[(n, what)])
             transpose_sum(bank, sources)
             bank_of[(n, what)] = bank
 
@@ -354,10 +367,10 @@ def tile_mylstm_v_kernel(
                 if n + GATES_AHEAD < N_TILES:
                     gates_first(n + GATES_AHEAD)
                 minus_one_times(n, "o_th", "o", th_of[n])
+                ring(n, "bracket_f")
                 times(n, "y", "i", by_unit_of[(n, "minus_dc")])
                 new_dz(n)
                 gradient(n, 3, "og", "o_th", -1)
-                ring(n, "bracket_f")
                 if more:
                     ring(n + 1, "og")
                 if multiplied > first_of_round:

@@ -361,7 +361,9 @@ def tile_mylstm_v_kernel(
                 elif more:
                     brackets(n + 1)
                 if multiplied > first_of_round:
-                    multiply(multiplied - 1)
+                    new_acc(multiplied - 1)
+                    multiply_gate(multiplied - 1, 0, True, False)
+                    multiply_gate(multiplied - 1, 1, False, False)
                 if n + 2 < N_TILES:
                     products(n + 2, nc.gpsimd)
                 if n + GATES_AHEAD < N_TILES:
@@ -373,11 +375,13 @@ def tile_mylstm_v_kernel(
                 gradient(n, 3, "og", "o_th", -1)
                 if more:
                     ring(n + 1, "og")
-                if multiplied > first_of_round:
-                    store(multiplied - 1)
                 minus_one_times(n, "w", "i", by_unit_of[(n, "y")])
                 if more:
                     ring(n + 1, "o")
+                if multiplied > first_of_round:
+                    multiply_gate(multiplied - 1, 2, False, False)
+                    multiply_gate(multiplied - 1, 3, False, True)
+                    store(multiplied - 1)
                 gradient_minus_one(n, 2, "c_tilde_sq", "y")
                 if more:
                     ring(n + 1, "i")

from contextlib import ExitStack

import concourse.mybir as mybir
from concourse.masks import make_identity

F32 = mybir.dt.float32
BF16 = mybir.dt.bfloat16
U32 = mybir.dt.uint32
U8 = mybir.dt.uint8
E4M3_X4 = mybir.dt.float8_e4m3fn_x4
E5M2_X4 = mybir.dt.float8_e5m2_x4
ACT = mybir.ActivationFunctionType
ALU = mybir.AluOpType

P = 128
PACK = 4
TOKENS, D, U = 2048, 512, 512
GATES = 4
N_TILES = TOKENS // P
LOAD_AHEAD = 4
GATES_AHEAD = 3
FIRST_MX_ROUND = GATES + 1
MX_TILES_A_ROUND = 2
RING = 5
SPLIT_FROM = 7
GPSIMD_UNITS = 256
FINE_TILES = 2
INHERITS = {
    "bracket_f": (0, "o"),
    "og": (1, "og"),
    "o": (1, "i"),
    "i": (1, "c_tilde_sq"),
    "c_tilde_sq": (1, "c_tilde"),
    "c_tilde": (1, "bracket_f"),
}
FIRST_BANKS = {(0, "og"): 0, (0, "o"): 1, (0, "i"): 2, (0, "c_tilde_sq"): 3, (0, "c_tilde"): 4}
SLOTS = 3

FLOPS = 2 * TOKENS * D * GATES * U
BYTES = 4 * TOKENS * GATES * U + 2 * 2 * TOKENS * U + 2 * GATES * D * U + 4 * TOKENS * D


def tile_mylstm_v_kernel(
    tc, inputs, h, c, w_i, u_i, b_i, w_f, u_f, b_f, w_c, u_c, b_c, w_o, u_o, b_o, z, grad_out, out
):
    nc = tc.nc
    weights = [w_i, w_f, w_c, w_o]

    with ExitStack() as pools:
        const = pools.enter_context(tc.tile_pool(name="const", bufs=1))
        w_pool = pools.enter_context(tc.tile_pool(name="w_pool", bufs=GATES))
        loads = pools.enter_context(tc.tile_pool(name="loads", bufs=LOAD_AHEAD + 1))
        by_token = pools.enter_context(tc.tile_pool(name="by_token", bufs=3))
        by_unit = pools.enter_context(tc.tile_pool(name="by_unit", bufs=2))
        quantised = pools.enter_context(tc.tile_pool(name="quantised", bufs=FIRST_MX_ROUND + 2))
        results = pools.enter_context(tc.tile_pool(name="results", bufs=MX_TILES_A_ROUND + 1))
        psum = pools.enter_context(tc.psum_pool(name="psum", bufs=1))

        ident_f32 = const.tile([P, P], F32)
        make_identity(nc, ident_f32[:])
        ident_bf16 = const.tile([P, P], BF16)
        make_identity(nc, ident_bf16[:])

        w_codes = const.tile([P, GATES, D], U32, align_bytes=64)
        w_scales = const.tile([P, GATES, D], U8, align_bytes=64)

        z_of, cg_of, sig_of, c_tilde_of, c_tilde_sq_of, prod_a_of, prod_bog_of, brackets_of = {}, {}, {}, {}, {}, {}, {}, {}
        c_new_of, th_of, th_sq_of, bank_of, by_unit_of, dz_of, mx_of, acc_of = {}, {}, {}, {}, {}, {}, {}, {}
        w_rows_of, wt_of, w_grouped_of, f_minus_one_of = {}, {}, {}, {}
        bank_number = {}

        def load(n):
            rows = slice(n * P, (n + 1) * P)
            z_sb = loads.tile([P, GATES * U], F32)
            cg = loads.tile([P, 2 * U], BF16)
            if n < FINE_TILES:
                nc.sync.dma_start(out=z_sb[:, 0:U], in_=z[rows, 0:U])
                nc.sync.dma_start(out=z_sb[:, 2 * U : 3 * U], in_=z[rows, 2 * U : 3 * U])
                nc.sync.dma_start(out=z_sb[:, U : 2 * U], in_=z[rows, U : 2 * U])
                nc.sync.dma_start(out=cg[:, 0:U], in_=c[rows, :])
                nc.sync.dma_start(out=z_sb[:, 3 * U : 4 * U], in_=z[rows, 3 * U : 4 * U])
            else:
                nc.sync.dma_start(out=z_sb[:, 0 : 2 * U], in_=z[rows, 0 : 2 * U])
                nc.sync.dma_start(out=cg[:, 0:U], in_=c[rows, :])
                nc.sync.dma_start(out=z_sb[:, 2 * U : 4 * U], in_=z[rows, 2 * U : 4 * U])
            nc.sync.dma_start(out=cg[:, U : 2 * U], in_=grad_out[rows, :])
            z_of[n], cg_of[n] = z_sb, cg

        def load_weights():
            for gate in range(GATES):
                w_rows = w_pool.tile([P, D // P, U], BF16)
                nc.sync.dma_start(out=w_rows[:], in_=weights[gate].rearrange("(j p) u -> p j u", p=P))
                w_rows_of[gate] = w_rows
                w_grouped = w_pool.tile([P, D, PACK], BF16, align_bytes=64)
                w_grouped_of[gate] = w_grouped

        def transpose_weights(gate, half):
            wt = psum.tile([P, PACK, 2 * P], BF16, tag="acc", bufs=2)
            for j in range(2):
                for t in range(PACK):
                    nc.tensor.transpose(
                        wt[:, t, j * P : (j + 1) * P],
                        w_rows_of[gate][:, 2 * half + j, t * P : (t + 1) * P],
                        ident_bf16[:],
                    )
            wt_of[(gate, half)] = wt

        def group_weights(gate, half):
            nc.scalar.copy(
                out=w_grouped_of[gate][:, half * 2 * P : (half + 1) * 2 * P, :],
                in_=wt_of[(gate, half)][:].rearrange("p t d -> p d t"),
            )

        def quantise_weights(gate):
            nc.vector.quantize_mx(
                out=w_codes[:, gate, :].bitcast(E4M3_X4),
                scales=w_scales[:, gate, :],
                in_=w_grouped_of[gate][:].rearrange("p d t -> p (d t)"),
            )

        def gates_first(n):
            z_sb = z_of[n]
            sig = by_token.tile([P, 3 * U], F32, bufs=GATES_AHEAD + 1)
            c_tilde = by_token.tile([P, U], F32)
            if n < FINE_TILES:
                nc.scalar.activation(out=sig[:, 0:U], in_=z_sb[:, 0:U], func=ACT.Sigmoid)
                nc.scalar.activation(out=c_tilde[:], in_=z_sb[:, 2 * U : 3 * U], func=ACT.Tanh)
                nc.scalar.activation(out=sig[:, U : 2 * U], in_=z_sb[:, U : 2 * U], func=ACT.Sigmoid)
            else:
                nc.scalar.activation(out=sig[:, 0 : 2 * U], in_=z_sb[:, 0 : 2 * U], func=ACT.Sigmoid)
                nc.scalar.activation(out=c_tilde[:], in_=z_sb[:, 2 * U : 3 * U], func=ACT.Tanh)
            sig_of[n], c_tilde_of[n] = sig, c_tilde

        def gate_o(n):
            nc.scalar.activation(out=sig_of[n][:, 2 * U : 3 * U], in_=z_of[n][:, 3 * U : 4 * U], func=ACT.Sigmoid)

        def gate_square(n):
            c_tilde_sq = by_token.tile([P, U], F32)
            nc.scalar.activation(out=c_tilde_sq[:], in_=c_tilde_of[n][:], func=ACT.Square)
            c_tilde_sq_of[n] = c_tilde_sq

        def gates_second(n):
            gate_o(n)
            gate_square(n)
            if n >= SPLIT_FROM:
                f_minus_one = by_token.tile([P, GPSIMD_UNITS], F32)
                nc.scalar.add(out=f_minus_one[:], in_=sig_of[n][:, 2 * U - GPSIMD_UNITS : 2 * U], add=-1.0)
                f_minus_one_of[n] = f_minus_one

        def slot(n):
            return "slot%d" % (n % SLOTS)

        def products(n, engine):
            sig = sig_of[n]
            prod_a = by_token.tile([P, U], F32, tag=slot(n), bufs=1, align_bytes=64)
            engine.tensor_tensor(out=prod_a[:], in0=sig[:, 0:U], in1=c_tilde_of[n][:], op=ALU.mult)
            prod_bog = by_token.tile([P, 2 * U], F32)
            if n < FINE_TILES:
                engine.tensor_tensor(out=prod_bog[:, 0:U], in0=sig[:, U : 2 * U], in1=cg_of[n][:, 0:U], op=ALU.mult)
            else:
                engine.tensor_tensor(out=prod_bog[:], in0=sig[:, U : 3 * U], in1=cg_of[n][:], op=ALU.mult)
            prod_a_of[n], prod_bog_of[n] = prod_a, prod_bog
            bracket_f = by_token.tile([P, U], F32)
            brackets_of[n] = bracket_f
            if n >= SPLIT_FROM:
                theirs = slice(U - GPSIMD_UNITS, U)
                engine.tensor_tensor(
                    out=bracket_f[:, theirs], in0=f_minus_one_of[n][:], in1=prod_bog[:, theirs], op=ALU.mult
                )

        def product_og(n):
            nc.vector.tensor_tensor(
                out=prod_bog_of[n][:, U : 2 * U], in0=sig_of[n][:, 2 * U : 3 * U], in1=cg_of[n][:, U : 2 * U], op=ALU.mult
            )

        def brackets(n):
            ours = U - GPSIMD_UNITS if n >= SPLIT_FROM else U
            nc.vector.scalar_tensor_tensor(
                out=brackets_of[n][:, 0:ours], in0=sig_of[n][:, U : U + ours], scalar=1.0,
                in1=prod_bog_of[n][:, 0:ours], op0=ALU.subtract, op1=ALU.mult,
            )

        def transpose_sum(bank, sources):
            for t in range(PACK):
                units = slice(t * P, (t + 1) * P)
                if len(sources) == 1:
                    nc.tensor.transpose(bank[:, t, :], sources[0][:, units], ident_f32[:])
                else:
                    for k, source in enumerate(sources):
                        nc.tensor.matmul(
                            out=bank[:, t, :], lhsT=source[:, units], rhs=ident_f32[:],
                            is_transpose=True, start=(k == 0), stop=(k == len(sources) - 1),
                        )

        def cell_sum(n):
            c_new = psum.tile([P, PACK, P], F32)
            transpose_sum(c_new, [prod_a_of[n][:], prod_bog_of[n][:, 0:U]])
            c_new_of[n] = c_new

        def ring(n, what):
            sig = sig_of[n]
            sources = {
                "og": lambda: [prod_bog_of[n][:, U : 2 * U]],
                "o": lambda: [sig[:, 2 * U : 3 * U]],
                "i": lambda: [sig[:, 0:U]],
                "c_tilde_sq": lambda: [c_tilde_sq_of[n][:]],
                "c_tilde": lambda: [c_tilde_of[n][:]],
                "bracket_f": lambda: [brackets_of[n][:]],
            }[what]()
            if (n, what) in FIRST_BANKS:
                bank_number[(n, what)] = FIRST_BANKS[(n, what)]
            else:
                tiles_back, heir_of = INHERITS[what]
                bank_number[(n, what)] = bank_number[(n - tiles_back, heir_of)]
            bank = psum.tile([P, PACK, P], F32, tag="ring%d" % bank_number[(n, what)])
            transpose_sum(bank, sources)
            bank_of[(n, what)] = bank

        def word_order(bank):
            return bank[:].rearrange("p t b -> p b t")

        def cell_tanh(n):
            th = by_unit.tile([P, P, PACK], F32)
            nc.scalar.activation(out=th[:], in_=word_order(c_new_of[n]), func=ACT.Tanh)
            th_sq = by_unit.tile([P, P, PACK], F32)
            nc.scalar.activation(out=th_sq[:], in_=th[:], func=ACT.Square)
            th_of[n], th_sq_of[n] = th, th_sq

        def minus_one_times(n, name, what, other):
            result = by_unit.tile([P, P, PACK], F32, tag=name)
            nc.vector.scalar_tensor_tensor(
                out=result[:], in0=word_order(bank_of[(n, what)]), scalar=1.0, in1=other[:],
                op0=ALU.subtract, op1=ALU.mult,
            )
            by_unit_of[(n, name)] = result

        def times(n, name, what, other):
            result = by_unit.tile([P, P, PACK], F32, tag=name)
            nc.vector.tensor_tensor(out=result[:], in0=word_order(bank_of[(n, what)]), in1=other[:], op=ALU.mult)
            by_unit_of[(n, name)] = result

        def minus_dc(n):
            result = by_unit.tile([P, P, PACK], F32, tag="minus_dc")
            nc.vector.scalar_tensor_tensor(
                out=result[:], in0=th_sq_of[n][:], scalar=1.0, in1=word_order(bank_of[(n, "og")]),
                op0=ALU.subtract, op1=ALU.mult,
            )
            by_unit_of[(n, "minus_dc")] = result

        def new_dz(n):
            dz = by_token.tile([P, GATES, P, PACK], BF16, tag=slot(n), bufs=1, align_bytes=64)
            dz_of[n] = dz

        def gradient_minus_one(n, gate, what, name):
            nc.vector.scalar_tensor_tensor(
                out=dz_of[n][:, gate], in0=word_order(bank_of[(n, what)]), scalar=1.0,
                in1=by_unit_of[(n, name)][:], op0=ALU.subtract, op1=ALU.mult,
            )

        def gradient(n, gate, what, name, sign):
            if sign > 0:
                nc.vector.tensor_tensor(
                    out=dz_of[n][:, gate], in0=word_order(bank_of[(n, what)]), in1=by_unit_of[(n, name)][:], op=ALU.mult
                )
            else:
                nc.vector.scalar_tensor_tensor(
                    out=dz_of[n][:, gate], in0=word_order(bank_of[(n, what)]), scalar=-1.0,
                    in1=by_unit_of[(n, name)][:], op0=ALU.mult, op1=ALU.mult,
                )

        def new_codes(n):
            dz_codes = quantised.tile([P, GATES, P], U32, align_bytes=64)
            dz_scales = quantised.tile([P, GATES, P], U8, align_bytes=64)
            mx_of[n] = (dz_codes, dz_scales)

        def quantise(n):
            new_codes(n)
            dz_codes, dz_scales = mx_of[n]
            nc.vector.quantize_mx(
                out=dz_codes[:].rearrange("p g b -> p (g b)").bitcast(E5M2_X4),
                scales=dz_scales[:].rearrange("p g b -> p (g b)"),
                in_=dz_of[n][:].rearrange("p g b t -> p (g b t)"),
            )

        def quantise_gate(n, gate):
            dz_codes, dz_scales = mx_of[n]
            nc.vector.quantize_mx(
                out=dz_codes[:, gate, :].bitcast(E5M2_X4),
                scales=dz_scales[:, gate, :],
                in_=dz_of[n][:, gate].rearrange("p b t -> p (b t)"),
            )

        def new_acc(n):
            acc = psum.tile([P, D], F32, tag="acc", bufs=2)
            acc_of[n] = acc

        def multiply_gate(n, gate, first, last):
            dz_codes, dz_scales = mx_of[n]
            nc.tensor.matmul_mx(
                out=acc_of[n][:],
                lhsT=dz_codes[:, gate, :].bitcast(E5M2_X4),
                lhsT_scale=dz_scales[:, gate, :],
                rhs=w_codes[:, gate, :].bitcast(E4M3_X4),
                rhs_scale=w_scales[:, gate, :],
                start=first,
                stop=last,
            )

        def multiply(n):
            new_acc(n)
            for gate in range(GATES):
                multiply_gate(n, gate, gate == 0, gate == GATES - 1)

        def store(n):
            out_rows = results.tile([P, D], F32)
            nc.scalar.copy(out=out_rows[:], in_=acc_of[n][:])
            nc.sync.dma_start(out=out[n * P : (n + 1) * P, :], in_=out_rows[:])

        with tc.manual_schedule():
            for n in range(LOAD_AHEAD):
                load(n)
            load_weights()
            gates_first(0)
            gate_o(0)
            products(0, nc.vector)
            cell_sum(0)
            product_og(0)
            gates_first(1)
            brackets(0)
            cell_tanh(0)
            for what in ("og", "o", "i"):
                ring(0, what)
            products(1, nc.vector)
            cell_sum(1)
            brackets(1)
            gate_o(1)
            gate_square(0)
            ring(0, "c_tilde_sq")
            gates_first(2)
            gates_second(2)
            gate_square(1)
            multiplied = 0
            for n in range(N_TILES):
                more = n + 1 < N_TILES
                if n + LOAD_AHEAD < N_TILES:
                    load(n + LOAD_AHEAD)
                if more:
                    cell_tanh(n + 1)
                ring(n, "c_tilde")
                first_of_round = multiplied
                if n >= FIRST_MX_ROUND:
                    multiplied = min(n, first_of_round + MX_TILES_A_ROUND)
                if multiplied > first_of_round + 1:
                    multiply(first_of_round)
                    store(first_of_round)
                minus_dc(n)
                if n >= 1:
                    quantise(n - 1)
                if n == 0:
                    product_og(1)
                elif more:
                    brackets(n + 1)
                if multiplied > first_of_round:
                    new_acc(multiplied - 1)
                    multiply_gate(multiplied - 1, 0, True, False)
                    multiply_gate(multiplied - 1, 1, False, False)
                if n + 2 < N_TILES:
                    products(n + 2, nc.gpsimd)
                if n + GATES_AHEAD < N_TILES:
                    gates_first(n + GATES_AHEAD)
                minus_one_times(n, "o_th", "o", th_of[n])
                ring(n, "bracket_f")
                times(n, "y", "i", by_unit_of[(n, "minus_dc")])
                new_dz(n)
                gradient(n, 3, "og", "o_th", -1)
                if more:
                    ring(n + 1, "og")
                minus_one_times(n, "w", "i", by_unit_of[(n, "y")])
                if more:
                    ring(n + 1, "o")
                if multiplied > first_of_round:
                    multiply_gate(multiplied - 1, 2, False, False)
                    multiply_gate(multiplied - 1, 3, False, True)
                    store(multiplied - 1)
                gradient_minus_one(n, 2, "c_tilde_sq", "y")
                if more:
                    ring(n + 1, "i")
                else:
                    new_codes(n)
                    quantise_gate(n, 3)
                gradient(n, 0, "c_tilde", "w", 1)
                if more:
                    ring(n + 1, "c_tilde_sq")
                else:
                    quantise_gate(n, 2)
                gradient(n, 1, "bracket_f", "minus_dc", 1)
                if 1 <= n <= GATES:
                    quantise_weights(n - 1)
                if n + GATES_AHEAD < N_TILES:
                    gates_second(n + GATES_AHEAD)
                if n + 2 < N_TILES:
                    cell_sum(n + 2)
                if n < GATES:
                    transpose_weights(n, 0)
                    transpose_weights(n, 1)
                    group_weights(n, 0)
                    group_weights(n, 1)
            last_tile = N_TILES - 1
            new_acc(last_tile)
            multiply_gate(last_tile, 3, True, False)
            multiply_gate(last_tile, 2, False, False)
            quantise_gate(last_tile, 0)
            multiply_gate(last_tile, 0, False, False)
            quantise_gate(last_tile, 1)
            multiply_gate(last_tile, 1, False, True)
            store(last_tile)
